import numpy as np
import ml_dtypes


def mxq(x, axis, fmt="e4m3"):
    dtype, down = {"e4m3": (ml_dtypes.float8_e4m3fn, 7), "e5m2": (ml_dtypes.float8_e5m2, 14)}[fmt]
    v = np.moveaxis(np.asarray(x, np.float32).astype(ml_dtypes.bfloat16).astype(np.float64), axis, -1)
    blocks = v.reshape(v.shape[:-1] + (-1, 32))
    amax = np.abs(blocks).max(-1, keepdims=True)
    byte = np.maximum(np.where(amax > 0, np.frexp(amax)[1] - 1 + 127, 0) - down, 1)
    scale = np.exp2(byte - 127.0)
    codes = (blocks / scale).astype(np.float32).astype(dtype).astype(np.float64)
    return np.moveaxis((codes * scale).reshape(v.shape), -1, axis)


WIDE = False


def mx_kscale(k):
    if not WIDE:
        return np.ones(k)
    levels = np.array([10, -10, 5, -5, 0])
    if k % 512:
        return np.exp2(np.random.permutation(np.resize(levels, k // 32))).repeat(32)
    a = np.empty((k // 512, 16))
    for p in range(k // 512):
        a[p, :8] = np.random.permutation(np.resize(levels, 8))
        for g in range(8):
            far = levels[np.abs(levels - a[p, g]) >= 10]
            a[p, g + 8] = far[np.random.randint(len(far))]
    return np.exp2(a.ravel()).repeat(32)


BF16 = ml_dtypes.bfloat16


def bf(x):
    return np.asarray(x, np.float32).astype(BF16)


def f64(x):
    return np.asarray(x).astype(np.float64)


B, C, T, V, OUT, REL, TS = 1, 512, 128, 32, 1024, 64, 16
TP = T + TS - 1
K = V * TS


def setup_inputs():
    s = mx_kscale(K)[::TS]
    t = mx_kscale(C)
    return {'x_pad': bf(np.random.standard_normal((B, C, TP, V)) * t[None, :, None, None] * s),
            'rel': bf(np.random.standard_normal((B, C * TS, V, V)) / np.sqrt(K) / s[:, None]),
            'A': bf(np.random.standard_normal((V, V)) * 0.7 / np.sqrt(K) / s[:, None]),
            'w3': bf(np.random.standard_normal((OUT, C)) / np.sqrt(C) / t),
            'b3': bf(np.random.standard_normal(OUT) * 0.3)}


def reference(x_pad, rel, A, w3, b3):
    adj = f64(rel) + f64(A)[None, None]
    W = adj.reshape(B, C, TS, V, V).transpose(0, 1, 3, 2, 4).reshape(B, C, K, V)
    xf = f64(x_pad)
    xw = np.stack([xf[:, :, k:k + T, :] for k in range(TS)], axis=-1).reshape(B, C, T, K)
    z = mxq(xw, 3, 'e4m3') @ mxq(W, 2, 'e4m3')
    y = mxq(f64(w3), 1, 'e4m3') @ mxq(z.reshape(B, C, T * V), 1, 'e4m3')
    return (y + f64(b3)[None, :, None]).reshape(B, OUT, T, V)

@@ -1,0 +1,301 @@
+from contextlib import ExitStack
+
+import concourse.mybir as mybir
+from concourse.masks import make_identity
+
+FLOPS = 2 * 512 * 128 * 512 * 32 + 2 * 1024 * 512 * 128 * 32
+
+BF16 = mybir.dt.bfloat16
+F32 = mybir.dt.float32
+U32 = mybir.dt.uint32
+U8 = mybir.dt.uint8
+FP8X4 = mybir.dt.float8_e4m3fn_x4
+ADD = mybir.AluOpType.add
+IDENTITY = mybir.ActivationFunctionType.Identity
+
+P = 128
+PACK = 4
+C = 512
+T = 128
+V = 32
+FRAMES = 143
+OUT = 1024
+PAIRS = V // 2
+KA = 8
+PITCH = 144
+NEED = T + KA
+COPIES = 2
+LOADS = KA // COPIES
+BLOCK = 128
+CHUNK = 32
+REL_CHUNK = 64
+GROUP = 8
+QUAD = 4
+N_TILE = 512
+T_STEP = N_TILE // V
+
+
+def tile_gccgc_pa_t_kernel(tc, x_pad, rel, A, w3, b3, out):
+    nc = tc.nc
+    n_groups = C // GROUP
+    groups_in_chunk = CHUNK // GROUP
+    groups_in_block = BLOCK // GROUP
+    n_chunks = C // CHUNK
+    run = (CHUNK - 1) * PITCH + NEED
+
+    out_words = out.rearrange("b o t i -> (b o t i)")
+    scratch = out_words[0 : PAIRS * COPIES * C * PITCH].rearrange("(blk x) -> blk x", blk=C // BLOCK)
+    rel_rows = rel[0].rearrange("(p r kh ka) (jp e) i -> r ka jp p kh (e i)", r=PACK, kh=2, ka=KA, e=2)
+    x_blocks = x_pad[0].rearrange("(p r) f v -> r p (f v)", r=PACK)
+
+    with ExitStack() as stack:
+        keep = stack.enter_context(tc.tile_pool(name="keep", bufs=1))
+        sort_pool = stack.enter_context(tc.tile_pool(name="sort", bufs=1))
+        win_pool = stack.enter_context(tc.tile_pool(name="win", bufs=2))
+        rel_pool = stack.enter_context(tc.tile_pool(name="rel", bufs=2))
+        w_pool = stack.enter_context(tc.tile_pool(name="wq", bufs=2))
+        x_pool = stack.enter_context(tc.tile_pool(name="xq", bufs=3))
+        acc_psum = stack.enter_context(tc.psum_pool(name="acc", bufs=4))
+        tr_psum = stack.enter_context(tc.psum_pool(name="tr", bufs=3))
+        stack.enter_context(tc.manual_schedule())
+
+        x_rows_of = {}
+        frames_of = {}
+        raw_of = {}
+        w_codes_of = {}
+        w_scales_of = {}
+        x_in_of = {}
+        x_codes_of = {}
+        x_scales_of = {}
+        acc_of = {}
+
+        def load_block(block):
+            x_rows_of[block] = sort_pool.tile([P, FRAMES * V], BF16, name="x_rows")
+            nc.sync.dma_start(
+                out=x_rows_of[block][:],
+                in_=x_blocks[block],
+            )
+
+        def sort_block(block):
+            sorted_rows = sort_pool.tile([P, PAIRS, PITCH + LOADS], F32)
+            nc.vector.memset(sorted_rows[:, :, FRAMES : PITCH + LOADS], 0.0)
+            nc.vector.tensor_copy(
+                out=sorted_rows[:, :, 0:FRAMES],
+                in_=x_rows_of[block][:].bitcast(F32).rearrange("c (f jp) -> c jp f", jp=PAIRS),
+            )
+            both = scratch[block].rearrange("(jp s c f) -> s c jp f", jp=PAIRS, s=COPIES, c=BLOCK)
+            for s in range(COPIES):
+                nc.sync.dma_start(out=both[s], in_=sorted_rows[:, :, LOADS * s : LOADS * s + PITCH])
+
+        def load_frames(chunk):
+            frames_of[chunk] = win_pool.tile([P, CHUNK * PITCH], F32, name="frames")
+            rows = scratch[chunk * CHUNK // BLOCK].rearrange("(row x) -> row x", row=PAIRS * COPIES)
+            for lo in range(LOADS):
+                first = (chunk * CHUNK % BLOCK) * PITCH + lo
+                nc.sync.dma_start(out=frames_of[chunk][lo:P:LOADS, 0:run], in_=rows[:, first : first + run])
+
+        def load_rel(part):
+            raw_of[part] = rel_pool.tile([P, REL_CHUNK, PACK, V], BF16, name="raw")
+            r, half = divmod(part, BLOCK // REL_CHUNK)
+            for ka in range(KA):
+                for kh in range(2):
+                    nc.sync.dma_start(
+                        out=raw_of[part][ka:P:KA, :, 2 * kh : 2 * kh + 2, :].rearrange("p c e i -> p c (e i)"),
+                        in_=rel_rows[r, ka, :, half * REL_CHUNK : (half + 1) * REL_CHUNK, kh, :],
+                    )
+
+        def weights(group):
+            chunk = group // groups_in_chunk
+            g0 = group % groups_in_chunk * GROUP
+            r0 = group * GROUP % REL_CHUNK
+            if g0 == 0:
+                w_codes_of[chunk] = w_pool.tile([P, CHUNK * V], U32, align_bytes=64, name="w_codes")
+                w_scales_of[chunk] = w_pool.tile([P, CHUNK * V], U8, align_bytes=64, name="w_scales")
+            w_in = w_pool.tile([P, GROUP, V, PACK], BF16, align_bytes=64)
+            nc.vector.tensor_tensor(
+                out=w_in[:],
+                in0=raw_of[group * GROUP // REL_CHUNK][:, r0 : r0 + GROUP].rearrange("p c r i -> p c i r"),
+                in1=a_words[:].rearrange("p i kh e -> p i (kh e)").unsqueeze(1).to_broadcast([P, GROUP, V, PACK]),
+                op=ADD,
+            )
+            cols = slice(g0 * V, (g0 + GROUP) * V)
+            nc.vector.quantize_mx(
+                out=w_codes_of[chunk][:, cols].bitcast(FP8X4),
+                scales=w_scales_of[chunk][:, cols],
+                in_=w_in[:].rearrange("p c i r -> p (c i r)"),
+            )
+
+        def windows(group):
+            g0 = group % groups_in_chunk * GROUP
+            blocks = frames_of[group // groups_in_chunk][:].rearrange("p (c u b) -> p c u b", c=CHUNK, b=KA)
+            x_in_of[group] = x_pool.tile([P, GROUP * T * PACK], BF16, align_bytes=64, name="x_in")
+            words = x_in_of[group][:].bitcast(F32).rearrange(
+                "p (c a odd b kh) -> p c a odd b kh", c=GROUP, odd=2, b=KA, kh=2
+            )
+            for odd in range(2):
+                nc.scalar.copy(
+                    out=words[:, :, :, odd],
+                    in_=blocks[:, g0 : g0 + GROUP, odd : odd + T // KA, :].rearrange(
+                        "p c (a kh) b -> p c a b kh", kh=2
+                    ),
+                )
+
+        def multiply(group):
+            x_codes = x_pool.tile([P, GROUP * T], U32, align_bytes=64)
+            x_scales = x_pool.tile([P, GROUP * T], U8, align_bytes=64)
+            nc.vector.quantize_mx(out=x_codes[:].bitcast(FP8X4), scales=x_scales[:], in_=x_in_of[group][:])
+            chunk = group // groups_in_chunk
+            for quad in range(GROUP // QUAD):
+                q0 = group % groups_in_chunk * GROUP + quad * QUAD
+                w_cols = slice(q0 * V, (q0 + QUAD) * V)
+                acc = acc_psum.tile([P, QUAD * QUAD * V], F32, tag="acc", name="acc")
+                acc_of[(group, quad)] = acc
+                for q in range(QUAD):
+                    t_cols = slice((quad * QUAD + q) * T, (quad * QUAD + q + 1) * T)
+                    nc.tensor.matmul_mx(
+                        out=acc[:, q * QUAD * V : (q + 1) * QUAD * V],
+                        lhsT=x_codes[:, t_cols].bitcast(FP8X4),
+                        lhsT_scale=x_scales[:, t_cols],
+                        rhs=w_codes_of[chunk][:, w_cols].bitcast(FP8X4),
+                        rhs_scale=w_scales_of[chunk][:, w_cols],
+                        start=True,
+                        stop=True,
+                    )
+
+        def collect(group):
+            for quad in range(GROUP // QUAD):
+                c0 = group * GROUP + quad * QUAD
+                own = acc_of[(group, quad)][:].rearrange("p (blk i) -> p blk i", i=V)[:, 0 : QUAD * QUAD : QUAD + 1, :]
+                if group // 2 % 2 == 0:
+                    nc.scalar.copy(out=z_sb[:, :, c0 : c0 + QUAD], in_=own.rearrange("p q i -> p i q"))
+                else:
+                    nc.vector.tensor_copy(out=z_sb[:, :, c0 : c0 + QUAD], in_=own.rearrange("p q i -> p i q"))
+
+        def turn(r):
+            for i0 in range(0, V, 8):
+                z_ps = tr_psum.tile([P, 8, T], BF16, tag="tr")
+                for i in range(8):
+                    nc.tensor.transpose(z_ps[:, i, :], z_sb[:, i0 + i, r * P : (r + 1) * P], ident[:])
+                if i0 < V // 2:
+                    nc.scalar.copy(out=z_t[:, r, :, i0 : i0 + 8], in_=z_ps[:].rearrange("p i t -> p t i"))
+                else:
+                    nc.vector.tensor_copy(out=z_t[:, r, :, i0 : i0 + 8], in_=z_ps[:].rearrange("p i t -> p t i"))
+
+        load_block(0)
+        ident = keep.tile([P, P], BF16)
+        make_identity(nc, ident[:])
+        a_raw = keep.tile([P, 2, V], BF16)
+        for ka in range(KA):
+            nc.sync.dma_start(
+                out=a_raw[ka:P:KA].rearrange("p e i -> p (e i)"),
+                in_=A.rearrange("(jp e) i -> jp (e i)", e=2),
+            )
+        b3_rows = keep.tile([P, P], BF16)
+        nc.vector.memset(b3_rows[:], 0.0)
+        nc.sync.dma_start(out=b3_rows[0 : OUT // P, :], in_=b3.rearrange("(a o) -> a o", o=P))
+        w3_codes = keep.tile([P, OUT], U32, align_bytes=64)
+        w3_scales = keep.tile([P, OUT], U8, align_bytes=64)
+        with tc.tile_pool(name="w3", bufs=1) as w3_pool:
+            w3_rows = w3_pool.tile([P, OUT // P, C], BF16)
+            nc.sync.dma_start(out=w3_rows[:], in_=w3.rearrange("(a p) c -> p a c", p=P))
+            load_rel(0)
+            sort_block(0)
+            load_frames(0)
+            load_rel(1)
+
+            b3_ps = tr_psum.tile([P, P], BF16, tag="tr")
+            nc.tensor.transpose(b3_ps[:], b3_rows[:], ident[:])
+            b3_cols = keep.tile([P, OUT // P], F32)
+            nc.vector.tensor_copy(out=b3_cols[:], in_=b3_ps[:, 0 : OUT // P])
+
+            w3_in = w3_pool.tile([P, OUT, PACK], BF16, align_bytes=64)
+            for two in range(OUT // P // 2):
+                w3_ps = tr_psum.tile([P, 2 * PACK, P], BF16, tag="tr")
+                for a in range(2):
+                    for r in range(PACK):
+                        nc.tensor.transpose(
+                            w3_ps[:, a * PACK + r, :], w3_rows[:, 2 * two + a, r:C:PACK], ident[:]
+                        )
+                nc.scalar.copy(
+                    out=w3_in[:, 2 * two * P : (2 * two + 2) * P, :].rearrange("p (a o) r -> p a o r", a=2),
+                    in_=w3_ps[:].rearrange("p (a r) o -> p a o r", a=2),
+                )
+            nc.vector.quantize_mx(
+                out=w3_codes[:].bitcast(FP8X4),
+                scales=w3_scales[:],
+                in_=w3_in[:].rearrange("p o r -> p (o r)"),
+            )
+
+        a_words = keep.tile([P, V, 2, 2], BF16)
+        for kh in range(2):
+            nc.vector.tensor_copy(out=a_words[:, :, kh, :], in_=a_raw[:].rearrange("p e i -> p i e"))
+        for group in range(groups_in_chunk):
+            weights(group)
+
+        late = stack.enter_context(tc.tile_pool(name="late", bufs=1))
+        z_pool = stack.enter_context(tc.tile_pool(name="zq", bufs=2))
+        y_pool = stack.enter_context(tc.tile_pool(name="y", bufs=4))
+        z_sb = keep.tile([P, V, C], BF16)
+        z_t = late.tile([P, PACK, T, V], BF16)
+
+        for s in range(n_groups + 3):
+            if s % groups_in_chunk == 0:
+                chunk = s // groups_in_chunk
+                if chunk + 1 < n_chunks:
+                    load_frames(chunk + 1)
+                if chunk % 2 == 1 and (chunk + 3) // 2 < C // REL_CHUNK:
+                    load_rel((chunk + 3) // 2)
+            if s % groups_in_block == 0 and s + groups_in_block < n_groups:
+                load_block(s // groups_in_block + 1)
+            if s < n_groups:
+                windows(s)
+            if 1 <= s <= n_groups:
+                multiply(s - 1)
+            if 2 <= s <= n_groups + 1:
+                collect(s - 2)
+            if s + groups_in_chunk < n_groups:
+                weights(s + groups_in_chunk)
+            if s % groups_in_block == groups_in_chunk and s + groups_in_block < n_groups:
+                sort_block(s // groups_in_block + 1)
+            if s >= 3 and (s - 2) % groups_in_block == 0:
+                turn((s - 3) // groups_in_block)
+
+        z_codes_of = {}
+        z_scales_of = {}
+
+        def quantise_z(step):
+            t_rows = slice(step * T_STEP, (step + 1) * T_STEP)
+            z_in = z_pool.tile([P, N_TILE, PACK], BF16, align_bytes=64)
+            nc.vector.tensor_copy(out=z_in[:], in_=z_t[:, :, t_rows, :].rearrange("p r t i -> p (t i) r"))
+            z_codes_of[step] = z_pool.tile([P, N_TILE], U32, align_bytes=64, name="z_codes")
+            z_scales_of[step] = z_pool.tile([P, N_TILE], U8, align_bytes=64, name="z_scales")
+            nc.vector.quantize_mx(
+                out=z_codes_of[step][:].bitcast(FP8X4),
+                scales=z_scales_of[step][:],
+                in_=z_in[:].rearrange("p n r -> p (n r)"),
+            )
+
+        n_steps = T // T_STEP
+        quantise_z(0)
+        for step in range(n_steps):
+            t_rows = slice(step * T_STEP, (step + 1) * T_STEP)
+            if step + 1 < n_steps:
+                quantise_z(step + 1)
+            for a in range(OUT // P):
+                o_cols = slice(a * P, (a + 1) * P)
+                y_ps = acc_psum.tile([P, N_TILE], F32, tag="acc")
+                nc.tensor.matmul_mx(
+                    out=y_ps[:],
+                    lhsT=w3_codes[:, o_cols].bitcast(FP8X4),
+                    lhsT_scale=w3_scales[:, o_cols],
+                    rhs=z_codes_of[step][:].bitcast(FP8X4),
+                    rhs_scale=z_scales_of[step][:],
+                    start=True,
+                    stop=True,
+                )
+                y = y_pool.tile([P, N_TILE], F32)
+                if a % 4 == 3:
+                    nc.vector.tensor_scalar_add(out=y[:], in0=y_ps[:], scalar1=b3_cols[:, a : a + 1])
+                else:
+                    nc.scalar.activation(out=y[:], in_=y_ps[:], func=IDENTITY, bias=b3_cols[:, a : a + 1])
+                nc.sync.dma_start(out=out[0, o_cols, t_rows, :].rearrange("o t i -> o (t i)"), in_=y[:])

@@ -18,19 +18,21 @@ PACK = 4
 C = 512
 T = 128
 V = 32
+TAPS = 16
 FRAMES = 143
 OUT = 1024
 PAIRS = V // 2
-KA = 8
 PITCH = 144
-NEED = T + KA
 COPIES = 2
-LOADS = KA // COPIES
+SHIFT = TAPS // COPIES
+LOADS = 4
 BLOCK = 128
-CHUNK = 32
-REL_CHUNK = 64
+SORT_PAIRS = 4
+CHUNK = 16
 GROUP = 8
 QUAD = 4
+K_ROWS = 4
+W_CHUNK = 32
 N_TILE = 512
 T_STEP = N_TILE // V
 
@@ -38,237 +40,290 @@ T_STEP = N_TILE // V
 def tile_gccgc_pa_t_kernel(tc, x_pad, rel, A, w3, b3, out):
     nc = tc.nc
     n_groups = C // GROUP
+    n_chunks = C // CHUNK
+    n_blocks = C // BLOCK
     groups_in_chunk = CHUNK // GROUP
     groups_in_block = BLOCK // GROUP
-    n_chunks = C // CHUNK
-    run = (CHUNK - 1) * PITCH + NEED
+    n_loads = TAPS // K_ROWS
+    n_ip = V // 2
+    run = (CHUNK - 1) * PITCH + T + 2
 
     out_words = out.rearrange("b o t i -> (b o t i)")
-    scratch = out_words[0 : PAIRS * COPIES * C * PITCH].rearrange("(blk x) -> blk x", blk=C // BLOCK)
-    rel_rows = rel[0].rearrange("(p r kh ka) (jp e) i -> r ka jp p kh (e i)", r=PACK, kh=2, ka=KA, e=2)
-    x_blocks = x_pad[0].rearrange("(p r) f v -> r p (f v)", r=PACK)
+    scratch = out_words[0 : PAIRS * COPIES * C * PITCH].rearrange("(blk x) -> blk x", blk=n_blocks)
+    rel_rows = rel[0].rearrange("(m r k) j i -> r m k (j i)", r=PACK, k=TAPS)
+    x_blocks = x_pad[0].rearrange("(m r) f v -> r m (f v)", r=PACK)
 
     with ExitStack() as stack:
-        keep = stack.enter_context(tc.tile_pool(name="keep", bufs=1))
-        sort_pool = stack.enter_context(tc.tile_pool(name="sort", bufs=1))
-        win_pool = stack.enter_context(tc.tile_pool(name="win", bufs=2))
-        rel_pool = stack.enter_context(tc.tile_pool(name="rel", bufs=2))
-        w_pool = stack.enter_context(tc.tile_pool(name="wq", bufs=2))
-        x_pool = stack.enter_context(tc.tile_pool(name="xq", bufs=3))
-        acc_psum = stack.enter_context(tc.psum_pool(name="acc", bufs=4))
-        tr_psum = stack.enter_context(tc.psum_pool(name="tr", bufs=3))
         stack.enter_context(tc.manual_schedule())
+        keep = stack.enter_context(tc.tile_pool(name="keep", bufs=1))
 
         x_rows_of = {}
         frames_of = {}
         raw_of = {}
+        wsum_of = {}
+        w_in_of = {}
+        w_ps_of = {}
         w_codes_of = {}
         w_scales_of = {}
-        x_in_of = {}
-        x_codes_of = {}
-        x_scales_of = {}
+        odd_of = {}
+        x_mx_of = {}
         acc_of = {}
+        z_sb_of = {}
 
-        def load_block(block):
-            x_rows_of[block] = sort_pool.tile([P, FRAMES * V], BF16, name="x_rows")
-            nc.sync.dma_start(
-                out=x_rows_of[block][:],
-                in_=x_blocks[block],
-            )
-
-        def sort_block(block):
-            sorted_rows = sort_pool.tile([P, PAIRS, PITCH + LOADS], F32)
-            nc.vector.memset(sorted_rows[:, :, FRAMES : PITCH + LOADS], 0.0)
-            nc.vector.tensor_copy(
-                out=sorted_rows[:, :, 0:FRAMES],
-                in_=x_rows_of[block][:].bitcast(F32).rearrange("c (f jp) -> c jp f", jp=PAIRS),
-            )
-            both = scratch[block].rearrange("(jp s c f) -> s c jp f", jp=PAIRS, s=COPIES, c=BLOCK)
-            for s in range(COPIES):
-                nc.sync.dma_start(out=both[s], in_=sorted_rows[:, :, LOADS * s : LOADS * s + PITCH])
-
-        def load_frames(chunk):
-            frames_of[chunk] = win_pool.tile([P, CHUNK * PITCH], F32, name="frames")
-            rows = scratch[chunk * CHUNK // BLOCK].rearrange("(row x) -> row x", row=PAIRS * COPIES)
-            for lo in range(LOADS):
-                first = (chunk * CHUNK % BLOCK) * PITCH + lo
-                nc.sync.dma_start(out=frames_of[chunk][lo:P:LOADS, 0:run], in_=rows[:, first : first + run])
-
-        def load_rel(part):
-            raw_of[part] = rel_pool.tile([P, REL_CHUNK, PACK, V], BF16, name="raw")
-            r, half = divmod(part, BLOCK // REL_CHUNK)
-            for ka in range(KA):
-                for kh in range(2):
-                    nc.sync.dma_start(
-                        out=raw_of[part][ka:P:KA, :, 2 * kh : 2 * kh + 2, :].rearrange("p c e i -> p c (e i)"),
-                        in_=rel_rows[r, ka, :, half * REL_CHUNK : (half + 1) * REL_CHUNK, kh, :],
-                    )
-
-        def weights(group):
-            chunk = group // groups_in_chunk
-            g0 = group % groups_in_chunk * GROUP
-            r0 = group * GROUP % REL_CHUNK
-            if g0 == 0:
-                w_codes_of[chunk] = w_pool.tile([P, CHUNK * V], U32, align_bytes=64, name="w_codes")
-                w_scales_of[chunk] = w_pool.tile([P, CHUNK * V], U8, align_bytes=64, name="w_scales")
-            w_in = w_pool.tile([P, GROUP, V, PACK], BF16, align_bytes=64)
-            nc.vector.tensor_tensor(
-                out=w_in[:],
-                in0=raw_of[group * GROUP // REL_CHUNK][:, r0 : r0 + GROUP].rearrange("p c r i -> p c i r"),
-                in1=a_words[:].rearrange("p i kh e -> p i (kh e)").unsqueeze(1).to_broadcast([P, GROUP, V, PACK]),
-                op=ADD,
-            )
-            cols = slice(g0 * V, (g0 + GROUP) * V)
-            nc.vector.quantize_mx(
-                out=w_codes_of[chunk][:, cols].bitcast(FP8X4),
-                scales=w_scales_of[chunk][:, cols],
-                in_=w_in[:].rearrange("p c i r -> p (c i r)"),
-            )
-
-        def windows(group):
-            g0 = group % groups_in_chunk * GROUP
-            blocks = frames_of[group // groups_in_chunk][:].rearrange("p (c u b) -> p c u b", c=CHUNK, b=KA)
-            x_in_of[group] = x_pool.tile([P, GROUP * T * PACK], BF16, align_bytes=64, name="x_in")
-            words = x_in_of[group][:].bitcast(F32).rearrange(
-                "p (c a odd b kh) -> p c a odd b kh", c=GROUP, odd=2, b=KA, kh=2
-            )
-            for odd in range(2):
-                nc.scalar.copy(
-                    out=words[:, :, :, odd],
-                    in_=blocks[:, g0 : g0 + GROUP, odd : odd + T // KA, :].rearrange(
-                        "p c (a kh) b -> p c a b kh", kh=2
-                    ),
-                )
-
-        def multiply(group):
-            x_codes = x_pool.tile([P, GROUP * T], U32, align_bytes=64)
-            x_scales = x_pool.tile([P, GROUP * T], U8, align_bytes=64)
-            nc.vector.quantize_mx(out=x_codes[:].bitcast(FP8X4), scales=x_scales[:], in_=x_in_of[group][:])
-            chunk = group // groups_in_chunk
-            for quad in range(GROUP // QUAD):
-                q0 = group % groups_in_chunk * GROUP + quad * QUAD
-                w_cols = slice(q0 * V, (q0 + QUAD) * V)
-                acc = acc_psum.tile([P, QUAD * QUAD * V], F32, tag="acc", name="acc")
-                acc_of[(group, quad)] = acc
-                for q in range(QUAD):
-                    t_cols = slice((quad * QUAD + q) * T, (quad * QUAD + q + 1) * T)
-                    nc.tensor.matmul_mx(
-                        out=acc[:, q * QUAD * V : (q + 1) * QUAD * V],
-                        lhsT=x_codes[:, t_cols].bitcast(FP8X4),
-                        lhsT_scale=x_scales[:, t_cols],
-                        rhs=w_codes_of[chunk][:, w_cols].bitcast(FP8X4),
-                        rhs_scale=w_scales_of[chunk][:, w_cols],
-                        start=True,
-                        stop=True,
-                    )
-
-        def collect(group):
-            for quad in range(GROUP // QUAD):
-                c0 = group * GROUP + quad * QUAD
-                own = acc_of[(group, quad)][:].rearrange("p (blk i) -> p blk i", i=V)[:, 0 : QUAD * QUAD : QUAD + 1, :]
-                if group // 2 % 2 == 0:
-                    nc.scalar.copy(out=z_sb[:, :, c0 : c0 + QUAD], in_=own.rearrange("p q i -> p i q"))
-                else:
-                    nc.vector.tensor_copy(out=z_sb[:, :, c0 : c0 + QUAD], in_=own.rearrange("p q i -> p i q"))
-
-        def turn(r):
-            for i0 in range(0, V, 8):
-                z_ps = tr_psum.tile([P, 8, T], BF16, tag="tr")
-                for i in range(8):
-                    nc.tensor.transpose(z_ps[:, i, :], z_sb[:, i0 + i, r * P : (r + 1) * P], ident[:])
-                if i0 < V // 2:
-                    nc.scalar.copy(out=z_t[:, r, :, i0 : i0 + 8], in_=z_ps[:].rearrange("p i t -> p t i"))
-                else:
-                    nc.vector.tensor_copy(out=z_t[:, r, :, i0 : i0 + 8], in_=z_ps[:].rearrange("p i t -> p t i"))
-
-        load_block(0)
-        ident = keep.tile([P, P], BF16)
+        ident = keep.tile([P, P], F32)
         make_identity(nc, ident[:])
-        a_raw = keep.tile([P, 2, V], BF16)
-        for ka in range(KA):
-            nc.sync.dma_start(
-                out=a_raw[ka:P:KA].rearrange("p e i -> p (e i)"),
-                in_=A.rearrange("(jp e) i -> jp (e i)", e=2),
-            )
-        b3_rows = keep.tile([P, P], BF16)
-        nc.vector.memset(b3_rows[:], 0.0)
-        nc.sync.dma_start(out=b3_rows[0 : OUT // P, :], in_=b3.rearrange("(a o) -> a o", o=P))
+        unsort = keep.tile([P, P], F32)
+        a_all = keep.tile([P, V * V], BF16)
         w3_codes = keep.tile([P, OUT], U32, align_bytes=64)
         w3_scales = keep.tile([P, OUT], U8, align_bytes=64)
-        with tc.tile_pool(name="w3", bufs=1) as w3_pool:
-            w3_rows = w3_pool.tile([P, OUT // P, C], BF16)
-            nc.sync.dma_start(out=w3_rows[:], in_=w3.rearrange("(a p) c -> p a c", p=P))
-            load_rel(0)
-            sort_block(0)
-            load_frames(0)
-            load_rel(1)
+        b3_rows = keep.tile([P, P], F32)
+        b3_cols = keep.tile([P, OUT // P], F32)
+        z_t = keep.tile([P, PACK, T, V], BF16)
 
-            b3_ps = tr_psum.tile([P, P], BF16, tag="tr")
-            nc.tensor.transpose(b3_ps[:], b3_rows[:], ident[:])
-            b3_cols = keep.tile([P, OUT // P], F32)
-            nc.vector.tensor_copy(out=b3_cols[:], in_=b3_ps[:, 0 : OUT // P])
+        with ExitStack() as first:
+            raw_pool = first.enter_context(tc.tile_pool(name="raw", bufs=4))
+            sort_pool = first.enter_context(tc.tile_pool(name="sort", bufs=3))
+            win_pool = first.enter_context(tc.tile_pool(name="win", bufs=3))
+            odd_pool = first.enter_context(tc.tile_pool(name="odd", bufs=2))
+            sum_pool = first.enter_context(tc.tile_pool(name="sum", bufs=1))
+            wq_pool = first.enter_context(tc.tile_pool(name="wq", bufs=5))
+            xq_pool = first.enter_context(tc.tile_pool(name="xq", bufs=3))
+            z_pool = first.enter_context(tc.tile_pool(name="z", bufs=2))
+            acc_psum = first.enter_context(tc.psum_pool(name="acc", bufs=3))
+            tw_psum = first.enter_context(tc.psum_pool(name="tw", bufs=3))
+            tz_psum = first.enter_context(tc.psum_pool(name="tz", bufs=2))
 
-            w3_in = w3_pool.tile([P, OUT, PACK], BF16, align_bytes=64)
-            for two in range(OUT // P // 2):
-                w3_ps = tr_psum.tile([P, 2 * PACK, P], BF16, tag="tr")
-                for a in range(2):
-                    for r in range(PACK):
-                        nc.tensor.transpose(
-                            w3_ps[:, a * PACK + r, :], w3_rows[:, 2 * two + a, r:C:PACK], ident[:]
+            def load_block(block):
+                x_rows_of[block] = raw_pool.tile([P, FRAMES * V], BF16, tag="raw", name="x_rows")
+                nc.sync.dma_start(out=x_rows_of[block][:], in_=x_blocks[block])
+
+            def sort_block(block):
+                both = scratch[block].rearrange("(jp s c f) -> s c jp f", jp=PAIRS, s=COPIES, c=BLOCK)
+                words = x_rows_of[block][:].bitcast(F32).rearrange("c (f jp) -> c jp f", jp=PAIRS)
+                for j0 in range(0, PAIRS, SORT_PAIRS):
+                    rows = sort_pool.tile([P, SORT_PAIRS, PITCH + SHIFT], F32, name="rows")
+                    nc.vector.memset(rows[:, :, FRAMES : PITCH + SHIFT], 0.0)
+                    nc.vector.tensor_copy(out=rows[:, :, 0:FRAMES], in_=words[:, j0 : j0 + SORT_PAIRS, :])
+                    for s in range(COPIES):
+                        nc.sync.dma_start(
+                            out=both[s, :, j0 : j0 + SORT_PAIRS, :], in_=rows[:, :, SHIFT * s : SHIFT * s + PITCH]
                         )
-                nc.scalar.copy(
-                    out=w3_in[:, 2 * two * P : (2 * two + 2) * P, :].rearrange("p (a o) r -> p a o r", a=2),
-                    in_=w3_ps[:].rearrange("p (a r) o -> p a o r", a=2),
+
+            def load_frames(chunk):
+                frames_of[chunk] = win_pool.tile([P, CHUNK * PITCH], F32, align_bytes=64, name="frames")
+                rows = scratch[chunk * CHUNK // BLOCK].rearrange("(row x) -> row x", row=PAIRS * COPIES)
+                for lo in range(LOADS):
+                    w0 = (chunk * CHUNK % BLOCK) * PITCH + 2 * lo
+                    nc.sync.dma_start(out=frames_of[chunk][lo:P:LOADS, 0:run], in_=rows[:, w0 : w0 + run])
+
+            def load_rel(block, part):
+                raw = raw_pool.tile([P, K_ROWS, V * V], BF16, tag="raw", name="raw")
+                raw_of[(block, part)] = raw
+                nc.sync.dma_start(out=raw[:], in_=rel_rows[block, :, part * K_ROWS : (part + 1) * K_ROWS, :])
+
+            def add_static(block, part):
+                if part == 0:
+                    wsum_of[block] = sum_pool.tile([P, TAPS * V * V], BF16, name="wsum")
+                sums = wsum_of[block][:].rearrange("c (jp k x) -> c k jp x", jp=PAIRS, k=TAPS)
+                nc.vector.tensor_tensor(
+                    out=sums[:, part * K_ROWS : (part + 1) * K_ROWS],
+                    in0=raw_of[(block, part)][:].rearrange("c k (jp x) -> c k jp x", jp=PAIRS),
+                    in1=a_all[:].rearrange("c (jp x) -> c jp x", jp=PAIRS).unsqueeze(1).to_broadcast([P, K_ROWS, PAIRS, 2 * V]),
+                    op=ADD,
                 )
-            nc.vector.quantize_mx(
-                out=w3_codes[:].bitcast(FP8X4),
-                scales=w3_scales[:],
-                in_=w3_in[:].rearrange("p o r -> p (o r)"),
+
+            def turn_weights(block, ip):
+                words = wsum_of[block][:].bitcast(F32).rearrange("c (p x) -> c p x", p=P)
+                w_ps = tw_psum.tile([P, PACK, P], F32, tag="tw", name="w_ps")
+                w_ps_of[(block, ip)] = w_ps
+                for r in range(PACK):
+                    nc.tensor.transpose(w_ps[:, r, :], words[:, :, r * n_ip + ip], ident[:])
+
+            def lay_weights(block, ip, on_vector):
+                if ip == 0:
+                    w_in_of[block] = sum_pool.tile([P, BLOCK, V, PACK], BF16, align_bytes=64, tag="w_in", name="w_in")
+                src = w_ps_of[(block, ip)][:].bitcast(BF16).rearrange("p r (c h) -> p c h r", h=2)
+                dst = w_in_of[block][:, :, 2 * ip : 2 * ip + 2, :]
+                if on_vector:
+                    nc.vector.tensor_copy(out=dst, in_=src)
+                else:
+                    nc.scalar.copy(out=dst, in_=src)
+
+            def quantise_weights(block, part):
+                key = block * (BLOCK // W_CHUNK) + part
+                w_codes_of[key] = wq_pool.tile([P, W_CHUNK * V], U32, align_bytes=64, name="w_codes")
+                w_scales_of[key] = wq_pool.tile([P, W_CHUNK * V], U8, align_bytes=64, name="w_scales")
+                nc.vector.quantize_mx(
+                    out=w_codes_of[key][:].bitcast(FP8X4),
+                    scales=w_scales_of[key][:],
+                    in_=w_in_of[block][:, part * W_CHUNK : (part + 1) * W_CHUNK].rearrange("p c i r -> p (c i r)"),
+                )
+
+            def odd_windows(group):
+                c0 = group % groups_in_chunk * GROUP
+                odd_of[group] = odd_pool.tile([P, GROUP, T], F32, align_bytes=64, name="odd")
+                src = frames_of[group // groups_in_chunk][:].rearrange("p (c f) -> p c f", c=CHUNK)
+                nc.scalar.copy(out=odd_of[group][:], in_=src[:, c0 : c0 + GROUP, 1 : T + 1])
+
+            def quantise_windows(group):
+                x_codes = xq_pool.tile([P, GROUP * T], U32, align_bytes=64, name="x_codes")
+                x_scales = xq_pool.tile([P, GROUP * T], U8, align_bytes=64, name="x_scales")
+                x_mx_of[group] = (x_codes, x_scales)
+                frames = frames_of[group // groups_in_chunk]
+                for c in range(GROUP):
+                    f0 = (group % groups_in_chunk * GROUP + c) * PITCH
+                    for odd in range(2):
+                        cols = slice(c * T + odd * T // 2, c * T + (odd + 1) * T // 2)
+                        src = odd_of[group][:, c, :] if odd else frames[:, f0 : f0 + T]
+                        nc.vector.quantize_mx(
+                            out=x_codes[:, cols].bitcast(FP8X4), scales=x_scales[:, cols], in_=src.bitcast(BF16)
+                        )
+
+            def multiply(group):
+                x_codes, x_scales = x_mx_of[group]
+                key = group * GROUP // W_CHUNK
+                for quad in range(GROUP // QUAD):
+                    q0 = group * GROUP % W_CHUNK + quad * QUAD
+                    w_cols = slice(q0 * V, (q0 + QUAD) * V)
+                    acc = acc_psum.tile([P, QUAD * QUAD * V], F32, tag="acc", name="acc")
+                    acc_of[(group, quad)] = acc
+                    for q in range(QUAD):
+                        t_cols = slice((quad * QUAD + q) * T, (quad * QUAD + q + 1) * T)
+                        nc.tensor.matmul_mx(
+                            out=acc[:, q * QUAD * V : (q + 1) * QUAD * V],
+                            lhsT=x_codes[:, t_cols].bitcast(FP8X4),
+                            lhsT_scale=x_scales[:, t_cols],
+                            rhs=w_codes_of[key][:, w_cols].bitcast(FP8X4),
+                            rhs_scale=w_scales_of[key][:, w_cols],
+                            start=True,
+                            stop=True,
+                        )
+
+            def collect(group):
+                block = group // groups_in_block
+                if group % groups_in_block == 0:
+                    z_sb_of[block] = z_pool.tile([P, BLOCK, V], BF16, name="z_sb")
+                for quad in range(GROUP // QUAD):
+                    c0 = group % groups_in_block * GROUP + quad * QUAD
+                    own = acc_of[(group, quad)][:].rearrange("p (blk i) -> p blk i", i=V)[:, 0 : QUAD * QUAD : QUAD + 1, :]
+                    dst = z_sb_of[block][:, c0 : c0 + QUAD, :]
+                    if group % groups_in_block < groups_in_block // 4:
+                        nc.scalar.copy(out=dst, in_=own)
+                    else:
+                        nc.vector.tensor_copy(out=dst, in_=own)
+
+            def turn(block):
+                z_words = z_sb_of[block][:].bitcast(F32)
+                for i0 in range(0, n_ip, 4):
+                    z_ps = tz_psum.tile([P, 4, T], F32, tag="tz")
+                    for i in range(4):
+                        nc.tensor.transpose(z_ps[:, i, :], z_words[:, :, i0 + i], unsort[:])
+                    nc.scalar.copy(
+                        out=z_t[:, block].bitcast(F32)[:, :, i0 : i0 + 4], in_=z_ps[:].rearrange("p i t -> p t i")
+                    )
+
+            def prepare_mix():
+                b3_in = raw_pool.tile([P, P], BF16, tag="raw", name="b3_in")
+                nc.sync.dma_start(out=b3_in[0 : OUT // P, :], in_=b3.rearrange("(a o) -> a o", o=P))
+                nc.vector.memset(b3_rows[:], 0.0)
+                nc.vector.tensor_copy(out=b3_rows[0 : OUT // P, :], in_=b3_in[0 : OUT // P, :])
+                b3_ps = tz_psum.tile([P, P], F32, tag="tz")
+                nc.tensor.transpose(b3_ps[:], b3_rows[:], ident[:])
+                nc.vector.tensor_copy(out=b3_cols[:], in_=b3_ps[:, 0 : OUT // P])
+                w3_rows = raw_pool.tile([P, OUT // P, C], BF16, tag="raw", name="w3_rows")
+                nc.sync.dma_start(out=w3_rows[:], in_=w3.rearrange("(a p) c -> p a c", p=P))
+                w3_in = sum_pool.tile([P, OUT, PACK], BF16, align_bytes=64, tag="w_in", name="w3_in")
+                w3_words = w3_in[:].bitcast(F32)
+                for two in range(OUT // P // 2):
+                    w3_ps = tz_psum.tile([P, 2, 2, P], F32, tag="tz")
+                    for a in range(2):
+                        for h in range(2):
+                            nc.tensor.transpose(
+                                w3_ps[:, a, h, :], w3_rows[:, 2 * two + a, :].bitcast(F32)[:, h : C // 2 : 2], ident[:]
+                            )
+                    nc.scalar.copy(
+                        out=w3_words[:, 2 * two * P : (2 * two + 2) * P, :].rearrange("p (a o) h -> p a o h", a=2),
+                        in_=w3_ps[:].rearrange("p a h o -> p a o h"),
+                    )
+                nc.vector.quantize_mx(
+                    out=w3_codes[:].bitcast(FP8X4), scales=w3_scales[:], in_=w3_in[:].rearrange("p o r -> p (o r)")
+                )
+
+            load_block(0)
+            nc.sync.dma_start(out=a_all[:], in_=A.rearrange("j i -> (j i)").partition_broadcast(P))
+            for part in range(n_loads - 1):
+                load_rel(0, part)
+            sort_block(0)
+            load_rel(0, n_loads - 1)
+            load_frames(0)
+            load_frames(1)
+            nc.vector.tensor_copy(
+                out=unsort[:].rearrange("p (w s) -> p s w", s=2), in_=ident[:].rearrange("p (s w) -> p s w", s=2)
             )
+            for part in range(n_loads):
+                add_static(0, part)
+            for ip in range(n_ip):
+                turn_weights(0, ip)
+                lay_weights(0, ip, ip % 2 == 1)
+                if ip == n_ip // 2:
+                    odd_windows(0)
+                    quantise_windows(0)
+            for part in range(BLOCK // W_CHUNK):
+                quantise_weights(0, part)
+            for part in range(n_loads - 1):
+                load_rel(1, part)
 
-        a_words = keep.tile([P, V, 2, 2], BF16)
-        for kh in range(2):
-            nc.vector.tensor_copy(out=a_words[:, :, kh, :], in_=a_raw[:].rearrange("p e i -> p i e"))
-        for group in range(groups_in_chunk):
-            weights(group)
+            for s in range(n_groups + 3):
+                block, g = divmod(s, groups_in_block)
+                more = block + 1 < n_blocks
+                if s % groups_in_chunk == 0 and s // groups_in_chunk + 2 < n_chunks:
+                    load_frames(s // groups_in_chunk + 2)
+                if 1 <= s < n_groups:
+                    odd_windows(s)
+                if 2 <= s <= n_groups:
+                    quantise_windows(s - 1)
+                if 1 <= s <= n_groups:
+                    multiply(s - 1)
+                if 2 <= s <= n_groups + 1:
+                    collect(s - 2)
+                if s >= 3 and (s - 2) % groups_in_block == 0:
+                    turn((s - 3) // groups_in_block)
+                if not more:
+                    if s == n_groups - groups_in_block + 4:
+                        prepare_mix()
+                    continue
+                if g < n_loads:
+                    add_static(block + 1, g)
+                    if g == 0:
+                        load_rel(block + 1, n_loads - 1)
+                turn_of = [max(0, (u - n_loads) * n_ip // 11) for u in (g, g + 1)]
+                for ip in range(turn_of[0], min(turn_of[1], n_ip)):
+                    turn_weights(block + 1, ip)
+                turned = [max(0, (u - n_loads) * n_ip // 11) for u in (g - 1, g)]
+                for ip in range(turned[0], min(turned[1], n_ip)):
+                    lay_weights(block + 1, ip, ip % 4 == 3)
+                if g == 1:
+                    load_block(block + 1)
+                if g == n_loads + 2:
+                    sort_block(block + 1)
+                if block + 2 < n_blocks and n_loads + 2 <= g < 2 * n_loads + 1:
+                    load_rel(block + 2, g - n_loads - 2)
+                if g == groups_in_block - 1:
+                    for part in range(BLOCK // W_CHUNK):
+                        quantise_weights(block + 1, part)
 
-        late = stack.enter_context(tc.tile_pool(name="late", bufs=1))
-        z_pool = stack.enter_context(tc.tile_pool(name="zq", bufs=2))
-        y_pool = stack.enter_context(tc.tile_pool(name="y", bufs=4))
-        z_sb = keep.tile([P, V, C], BF16)
-        z_t = late.tile([P, PACK, T, V], BF16)
-
-        for s in range(n_groups + 3):
-            if s % groups_in_chunk == 0:
-                chunk = s // groups_in_chunk
-                if chunk + 1 < n_chunks:
-                    load_frames(chunk + 1)
-                if chunk % 2 == 1 and (chunk + 3) // 2 < C // REL_CHUNK:
-                    load_rel((chunk + 3) // 2)
-            if s % groups_in_block == 0 and s + groups_in_block < n_groups:
-                load_block(s // groups_in_block + 1)
-            if s < n_groups:
-                windows(s)
-            if 1 <= s <= n_groups:
-                multiply(s - 1)
-            if 2 <= s <= n_groups + 1:
-                collect(s - 2)
-            if s + groups_in_chunk < n_groups:
-                weights(s + groups_in_chunk)
-            if s % groups_in_block == groups_in_chunk and s + groups_in_block < n_groups:
-                sort_block(s // groups_in_block + 1)
-            if s >= 3 and (s - 2) % groups_in_block == 0:
-                turn((s - 3) // groups_in_block)
-
+        zq_pool = stack.enter_context(tc.tile_pool(name="zq", bufs=2))
+        y_pool = stack.enter_context(tc.tile_pool(name="y", bufs=8))
+        y_psum = stack.enter_context(tc.psum_pool(name="y_ps", bufs=6))
         z_codes_of = {}
         z_scales_of = {}
 
         def quantise_z(step):
             t_rows = slice(step * T_STEP, (step + 1) * T_STEP)
-            z_in = z_pool.tile([P, N_TILE, PACK], BF16, align_bytes=64)
+            z_in = zq_pool.tile([P, N_TILE, PACK], BF16, align_bytes=64)
             nc.vector.tensor_copy(out=z_in[:], in_=z_t[:, :, t_rows, :].rearrange("p r t i -> p (t i) r"))
-            z_codes_of[step] = z_pool.tile([P, N_TILE], U32, align_bytes=64, name="z_codes")
-            z_scales_of[step] = z_pool.tile([P, N_TILE], U8, align_bytes=64, name="z_scales")
+            z_codes_of[step] = zq_pool.tile([P, N_TILE], U32, align_bytes=64, name="z_codes")
+            z_scales_of[step] = zq_pool.tile([P, N_TILE], U8, align_bytes=64, name="z_scales")
             nc.vector.quantize_mx(
                 out=z_codes_of[step][:].bitcast(FP8X4),
                 scales=z_scales_of[step][:],
@@ -283,7 +338,7 @@ def tile_gccgc_pa_t_kernel(tc, x_pad, rel, A, w3, b3, out):
                 quantise_z(step + 1)
             for a in range(OUT // P):
                 o_cols = slice(a * P, (a + 1) * P)
-                y_ps = acc_psum.tile([P, N_TILE], F32, tag="acc")
+                y_ps = y_psum.tile([P, N_TILE], F32, tag="y_ps")
                 nc.tensor.matmul_mx(
                     out=y_ps[:],
                     lhsT=w3_codes[:, o_cols].bitcast(FP8X4),
@@ -294,7 +349,7 @@ def tile_gccgc_pa_t_kernel(tc, x_pad, rel, A, w3, b3, out):
                     stop=True,
                 )
                 y = y_pool.tile([P, N_TILE], F32)
-                if a % 4 == 3:
+                if a % 3 == 1:
                     nc.vector.tensor_scalar_add(out=y[:], in0=y_ps[:], scalar1=b3_cols[:, a : a + 1])
                 else:
                     nc.scalar.activation(out=y[:], in_=y_ps[:], func=IDENTITY, bias=b3_cols[:, a : a + 1])

@@ -31,6 +31,7 @@ SORT_PAIRS = 4
 CHUNK = 16
 GROUP = 8
 QUAD = 4
+HALF = V // 2
 K_ROWS = 4
 W_CHUNK = 32
 N_TILE = 512
@@ -68,7 +69,9 @@ def tile_gccgc_pa_t_kernel(tc, x_pad, rel, A, w3, b3, out):
         odd_of = {}
         x_mx_of = {}
         acc_of = {}
+        mix = {}
         z_sb_of = {}
+        z_ps_of = {}
 
         ident = keep.tile([P, P], F32)
         make_identity(nc, ident[:])
@@ -82,25 +85,28 @@ def tile_gccgc_pa_t_kernel(tc, x_pad, rel, A, w3, b3, out):
 
         with ExitStack() as first:
             raw_pool = first.enter_context(tc.tile_pool(name="raw", bufs=4))
-            sort_pool = first.enter_context(tc.tile_pool(name="sort", bufs=3))
+            row_pool = first.enter_context(tc.tile_pool(name="row", bufs=1))
+            sort_pool = first.enter_context(tc.tile_pool(name="sort", bufs=2))
             win_pool = first.enter_context(tc.tile_pool(name="win", bufs=3))
-            odd_pool = first.enter_context(tc.tile_pool(name="odd", bufs=2))
-            sum_pool = first.enter_context(tc.tile_pool(name="sum", bufs=1))
-            wq_pool = first.enter_context(tc.tile_pool(name="wq", bufs=5))
-            xq_pool = first.enter_context(tc.tile_pool(name="xq", bufs=3))
+            odd_pool = first.enter_context(tc.tile_pool(name="odd", bufs=3))
+            sum_pool = first.enter_context(tc.tile_pool(name="sum", bufs=2))
+            win_pool_w = first.enter_context(tc.tile_pool(name="w_in", bufs=1))
+            wq_pool = first.enter_context(tc.tile_pool(name="wq", bufs=4))
+            xq_pool = first.enter_context(tc.tile_pool(name="xq", bufs=2))
             z_pool = first.enter_context(tc.tile_pool(name="z", bufs=2))
             acc_psum = first.enter_context(tc.psum_pool(name="acc", bufs=3))
             tw_psum = first.enter_context(tc.psum_pool(name="tw", bufs=3))
             tz_psum = first.enter_context(tc.psum_pool(name="tz", bufs=2))
 
             def load_block(block):
-                x_rows_of[block] = raw_pool.tile([P, FRAMES * V], BF16, tag="raw", name="x_rows")
+                x_rows_of[block] = row_pool.tile([P, FRAMES * V], BF16, name="x_rows")
                 nc.sync.dma_start(out=x_rows_of[block][:], in_=x_blocks[block])
 
-            def sort_block(block):
+            def sort_block(block, parts):
                 both = scratch[block].rearrange("(jp s c f) -> s c jp f", jp=PAIRS, s=COPIES, c=BLOCK)
                 words = x_rows_of[block][:].bitcast(F32).rearrange("c (f jp) -> c jp f", jp=PAIRS)
-                for j0 in range(0, PAIRS, SORT_PAIRS):
+                for part in parts:
+                    j0 = part * SORT_PAIRS
                     rows = sort_pool.tile([P, SORT_PAIRS, PITCH + SHIFT], F32, name="rows")
                     nc.vector.memset(rows[:, :, FRAMES : PITCH + SHIFT], 0.0)
                     nc.vector.tensor_copy(out=rows[:, :, 0:FRAMES], in_=words[:, j0 : j0 + SORT_PAIRS, :])
@@ -121,27 +127,32 @@ def tile_gccgc_pa_t_kernel(tc, x_pad, rel, A, w3, b3, out):
                 raw_of[(block, part)] = raw
                 nc.sync.dma_start(out=raw[:], in_=rel_rows[block, :, part * K_ROWS : (part + 1) * K_ROWS, :])
 
-            def add_static(block, part):
+            def add_static(block, half, part):
                 if part == 0:
-                    wsum_of[block] = sum_pool.tile([P, TAPS * V * V], BF16, name="wsum")
-                sums = wsum_of[block][:].rearrange("c (jp k x) -> c k jp x", jp=PAIRS, k=TAPS)
-                nc.vector.tensor_tensor(
-                    out=sums[:, part * K_ROWS : (part + 1) * K_ROWS],
-                    in0=raw_of[(block, part)][:].rearrange("c k (jp x) -> c k jp x", jp=PAIRS),
-                    in1=a_all[:].rearrange("c (jp x) -> c jp x", jp=PAIRS).unsqueeze(1).to_broadcast([P, K_ROWS, PAIRS, 2 * V]),
-                    op=ADD,
-                )
+                    wsum_of[(block, half)] = sum_pool.tile([P, TAPS * V * HALF], BF16, name="wsum")
+                sums = wsum_of[(block, half)][:].rearrange("c (jp k e i) -> c e k jp i", jp=PAIRS, k=TAPS, e=2)
+                raw = raw_of[(block, part)][:].rearrange("c k (jp e i) -> c e k jp i", jp=PAIRS, e=2)
+                static = a_all[:].rearrange("c (jp e i) -> c e jp i", jp=PAIRS, e=2)
+                i_cols = slice(half * HALF, (half + 1) * HALF)
+                for e in range(2):
+                    nc.vector.tensor_tensor(
+                        out=sums[:, e, part * K_ROWS : (part + 1) * K_ROWS],
+                        in0=raw[:, e, :, :, i_cols],
+                        in1=static[:, e, :, i_cols].unsqueeze(1).to_broadcast([P, K_ROWS, PAIRS, HALF]),
+                        op=ADD,
+                    )
 
             def turn_weights(block, ip):
-                words = wsum_of[block][:].bitcast(F32).rearrange("c (p x) -> c p x", p=P)
+                half, word = divmod(ip, HALF // 2)
+                words = wsum_of[(block, half)][:].bitcast(F32).rearrange("c (p x) -> c p x", p=P)
                 w_ps = tw_psum.tile([P, PACK, P], F32, tag="tw", name="w_ps")
                 w_ps_of[(block, ip)] = w_ps
                 for r in range(PACK):
-                    nc.tensor.transpose(w_ps[:, r, :], words[:, :, r * n_ip + ip], ident[:])
+                    nc.tensor.transpose(w_ps[:, r, :], words[:, :, r * HALF // 2 + word], ident[:])
 
             def lay_weights(block, ip, on_vector):
                 if ip == 0:
-                    w_in_of[block] = sum_pool.tile([P, BLOCK, V, PACK], BF16, align_bytes=64, tag="w_in", name="w_in")
+                    w_in_of[block] = win_pool_w.tile([P, BLOCK, V, PACK], BF16, align_bytes=64, tag="w_in", name="w_in")
                 src = w_ps_of[(block, ip)][:].bitcast(BF16).rearrange("p r (c h) -> p c h r", h=2)
                 dst = w_in_of[block][:, :, 2 * ip : 2 * ip + 2, :]
                 if on_vector:
@@ -207,110 +218,154 @@ def tile_gccgc_pa_t_kernel(tc, x_pad, rel, A, w3, b3, out):
                     c0 = group % groups_in_block * GROUP + quad * QUAD
                     own = acc_of[(group, quad)][:].rearrange("p (blk i) -> p blk i", i=V)[:, 0 : QUAD * QUAD : QUAD + 1, :]
                     dst = z_sb_of[block][:, c0 : c0 + QUAD, :]
-                    if group % groups_in_block < groups_in_block // 4:
-                        nc.scalar.copy(out=dst, in_=own)
-                    else:
-                        nc.vector.tensor_copy(out=dst, in_=own)
+                    nc.scalar.copy(out=dst, in_=own)
 
-            def turn(block):
+            def turn(block, quarter):
                 z_words = z_sb_of[block][:].bitcast(F32)
-                for i0 in range(0, n_ip, 4):
-                    z_ps = tz_psum.tile([P, 4, T], F32, tag="tz")
-                    for i in range(4):
-                        nc.tensor.transpose(z_ps[:, i, :], z_words[:, :, i0 + i], unsort[:])
-                    nc.scalar.copy(
-                        out=z_t[:, block].bitcast(F32)[:, :, i0 : i0 + 4], in_=z_ps[:].rearrange("p i t -> p t i")
-                    )
+                z_ps = tz_psum.tile([P, 4, T], F32, tag="tz", name="z_ps")
+                z_ps_of[(block, quarter)] = z_ps
+                for i in range(4):
+                    nc.tensor.transpose(z_ps[:, i, :], z_words[:, :, 4 * quarter + i], unsort[:])
 
-            def prepare_mix():
-                b3_in = raw_pool.tile([P, P], BF16, tag="raw", name="b3_in")
-                nc.sync.dma_start(out=b3_in[0 : OUT // P, :], in_=b3.rearrange("(a o) -> a o", o=P))
-                nc.vector.memset(b3_rows[:], 0.0)
-                nc.vector.tensor_copy(out=b3_rows[0 : OUT // P, :], in_=b3_in[0 : OUT // P, :])
-                b3_ps = tz_psum.tile([P, P], F32, tag="tz")
-                nc.tensor.transpose(b3_ps[:], b3_rows[:], ident[:])
-                nc.vector.tensor_copy(out=b3_cols[:], in_=b3_ps[:, 0 : OUT // P])
-                w3_rows = raw_pool.tile([P, OUT // P, C], BF16, tag="raw", name="w3_rows")
-                nc.sync.dma_start(out=w3_rows[:], in_=w3.rearrange("(a p) c -> p a c", p=P))
-                w3_in = sum_pool.tile([P, OUT, PACK], BF16, align_bytes=64, tag="w_in", name="w3_in")
-                w3_words = w3_in[:].bitcast(F32)
-                for two in range(OUT // P // 2):
-                    w3_ps = tz_psum.tile([P, 2, 2, P], F32, tag="tz")
-                    for a in range(2):
-                        for h in range(2):
-                            nc.tensor.transpose(
-                                w3_ps[:, a, h, :], w3_rows[:, 2 * two + a, :].bitcast(F32)[:, h : C // 2 : 2], ident[:]
-                            )
-                    nc.scalar.copy(
-                        out=w3_words[:, 2 * two * P : (2 * two + 2) * P, :].rearrange("p (a o) h -> p a o h", a=2),
-                        in_=w3_ps[:].rearrange("p a h o -> p a o h"),
-                    )
-                nc.vector.quantize_mx(
-                    out=w3_codes[:].bitcast(FP8X4), scales=w3_scales[:], in_=w3_in[:].rearrange("p o r -> p (o r)")
+            def spread(block, quarter):
+                nc.scalar.copy(
+                    out=z_t[:, block].bitcast(F32)[:, :, 4 * quarter : 4 * quarter + 4],
+                    in_=z_ps_of[(block, quarter)][:].rearrange("p i t -> p t i"),
                 )
+
+            def load_mix():
+                mix["b3"] = raw_pool.tile([P, P], BF16, tag="raw", name="b3_in")
+                nc.sync.dma_start(out=mix["b3"][0 : OUT // P, :], in_=b3.rearrange("(a o) -> a o", o=P))
+                mix["w3"] = raw_pool.tile([P, OUT // P, C], BF16, tag="raw", name="w3_rows")
+                nc.sync.dma_start(out=mix["w3"][:], in_=w3.rearrange("(a p) c -> p a c", p=P))
+
+            turning = {}
+            for step in range((n_blocks - 1) * groups_in_block):
+                u = step % groups_in_block
+                if step < n_ip // 2:
+                    turning[step] = [2 * u - 8, 2 * u - 7] if u >= n_loads else []
+                else:
+                    turning[step] = [u]
+
+            def turn_mix(two):
+                w3_ps = tz_psum.tile([P, 2, 2, P], F32, tag="tz", name="w3_ps")
+                mix[two] = w3_ps
+                for a in range(2):
+                    for h in range(2):
+                        nc.tensor.transpose(
+                            w3_ps[:, a, h, :], mix["w3"][:, 2 * two + a, :].bitcast(F32)[:, h : C // 2 : 2], ident[:]
+                        )
+
+            def lay_mix(two):
+                if two == 0:
+                    mix["in"] = win_pool_w.tile([P, OUT, PACK], BF16, align_bytes=64, tag="w_in", name="w3_in")
+                nc.scalar.copy(
+                    out=mix["in"][:].bitcast(F32)[:, 2 * two * P : (2 * two + 2) * P, :].rearrange(
+                        "p (a o) h -> p a o h", a=2
+                    ),
+                    in_=mix[two][:].rearrange("p a h o -> p a o h"),
+                )
+
+            def quantise_mix():
+                nc.vector.quantize_mx(
+                    out=w3_codes[:].bitcast(FP8X4), scales=w3_scales[:], in_=mix["in"][:].rearrange("p o r -> p (o r)")
+                )
+
+            def turn_bias():
+                nc.vector.memset(b3_rows[:], 0.0)
+                nc.vector.tensor_copy(out=b3_rows[0 : OUT // P, :], in_=mix["b3"][0 : OUT // P, :])
+                mix["b3_ps"] = tz_psum.tile([P, P], F32, tag="tz", name="b3_ps")
+                nc.tensor.transpose(mix["b3_ps"][:], b3_rows[:], ident[:])
+
+            def spread_bias():
+                nc.vector.tensor_copy(out=b3_cols[:], in_=mix["b3_ps"][:, 0 : OUT // P])
+
+            turning = {}
+            for step in range((n_blocks - 1) * groups_in_block):
+                u = step % groups_in_block
+                if step < n_ip // 2:
+                    turning[step] = [2 * u - 8, 2 * u - 7] if u >= n_loads else []
+                else:
+                    turning[step] = [u]
 
             load_block(0)
             nc.sync.dma_start(out=a_all[:], in_=A.rearrange("j i -> (j i)").partition_broadcast(P))
-            for part in range(n_loads - 1):
+            load_rel(0, 0)
+            sort_block(0, range(PAIRS // SORT_PAIRS))
+            for part in range(1, n_loads):
                 load_rel(0, part)
-            sort_block(0)
-            load_rel(0, n_loads - 1)
             load_frames(0)
             load_frames(1)
             nc.vector.tensor_copy(
                 out=unsort[:].rearrange("p (w s) -> p s w", s=2), in_=ident[:].rearrange("p (s w) -> p s w", s=2)
             )
-            for part in range(n_loads):
-                add_static(0, part)
-            for ip in range(n_ip):
+            for half in range(2):
+                for part in range(n_loads):
+                    add_static(0, half, part)
+                    if half == 1:
+                        load_rel(1, part)
+                        for ip in range(2 * part, 2 * part + 2):
+                            turn_weights(0, ip)
+                            lay_weights(0, ip, ip % 2 == 1)
+            for ip in range(n_ip // 2, n_ip):
                 turn_weights(0, ip)
                 lay_weights(0, ip, ip % 2 == 1)
-                if ip == n_ip // 2:
-                    odd_windows(0)
-                    quantise_windows(0)
-            for part in range(BLOCK // W_CHUNK):
-                quantise_weights(0, part)
-            for part in range(n_loads - 1):
-                load_rel(1, part)
+            odd_windows(0)
+            odd_windows(1)
 
-            for s in range(n_groups + 3):
+            for s in range(n_groups + 4):
                 block, g = divmod(s, groups_in_block)
-                more = block + 1 < n_blocks
+                inside = s < n_groups
                 if s % groups_in_chunk == 0 and s // groups_in_chunk + 2 < n_chunks:
                     load_frames(s // groups_in_chunk + 2)
-                if 1 <= s < n_groups:
-                    odd_windows(s)
-                if 2 <= s <= n_groups:
-                    quantise_windows(s - 1)
+                if s >= 1:
+                    for ip in turning.get(s - 1, []):
+                        lay_weights((s - 1) // groups_in_block + 1, ip, False)
+                if s + 2 < n_groups:
+                    odd_windows(s + 2)
+                if inside:
+                    quantise_windows(s)
+                    if g < 2:
+                        for part in range(2 * g, 2 * g + 2):
+                            quantise_weights(block, part)
+                    multiply(s)
+                if block == 0 and g < n_loads:
+                    add_static(1, 0, g)
+                if block == 0 and n_loads <= g < 2 * n_loads:
+                    add_static(1, 1, g - n_loads)
+                    load_rel(2, g - n_loads)
+                if block > 0 and block + 1 < n_blocks and g < 2 * n_loads and g % 2 == 0:
+                    add_static(block + 1, 1, g // 2)
+                    if block + 2 < n_blocks:
+                        load_rel(block + 2, g // 2)
+                if block + 2 < n_blocks and g >= 2 * n_loads and g % 2 == 0:
+                    add_static(block + 2, 0, g // 2 - n_loads)
                 if 1 <= s <= n_groups:
-                    multiply(s - 1)
-                if 2 <= s <= n_groups + 1:
-                    collect(s - 2)
-                if s >= 3 and (s - 2) % groups_in_block == 0:
-                    turn((s - 3) // groups_in_block)
-                if not more:
-                    if s == n_groups - groups_in_block + 4:
-                        prepare_mix()
-                    continue
-                if g < n_loads:
-                    add_static(block + 1, g)
-                    if g == 0:
-                        load_rel(block + 1, n_loads - 1)
-                turn_of = [max(0, (u - n_loads) * n_ip // 11) for u in (g, g + 1)]
-                for ip in range(turn_of[0], min(turn_of[1], n_ip)):
+                    collect(s - 1)
+                for ip in turning.get(s, []):
                     turn_weights(block + 1, ip)
-                turned = [max(0, (u - n_loads) * n_ip // 11) for u in (g - 1, g)]
-                for ip in range(turned[0], min(turned[1], n_ip)):
-                    lay_weights(block + 1, ip, ip % 4 == 3)
-                if g == 1:
+                if block > 0 and 2 <= g < 4:
+                    for quarter in range(2 * g - 4, 2 * g - 2):
+                        spread(block - 1, quarter)
+                if block > 0 and 1 <= g < 3:
+                    for quarter in range(2 * g - 2, 2 * g):
+                        turn(block - 1, quarter)
+                if g == 1 and block + 1 < n_blocks:
                     load_block(block + 1)
-                if g == n_loads + 2:
-                    sort_block(block + 1)
-                if block + 2 < n_blocks and n_loads + 2 <= g < 2 * n_loads + 1:
-                    load_rel(block + 2, g - n_loads - 2)
-                if g == groups_in_block - 1:
-                    for part in range(BLOCK // W_CHUNK):
-                        quantise_weights(block + 1, part)
+                if 4 <= g < 4 + PAIRS // SORT_PAIRS and block + 1 < n_blocks:
+                    sort_block(block + 1, [g - 4])
+                if block == n_blocks - 1:
+                    if g == 0:
+                        load_mix()
+                    if 6 <= g < 10:
+                        lay_mix(g - 6)
+                    if 5 <= g < 9:
+                        turn_mix(g - 5)
+                    if g == 10:
+                        quantise_mix()
+                        turn_bias()
+                    if g == 11:
+                        spread_bias()
 
         zq_pool = stack.enter_context(tc.tile_pool(name="zq", bufs=2))
         y_pool = stack.enter_context(tc.tile_pool(name="y", bufs=8))

@@ -28,9 +28,10 @@ SHIFT = TAPS // COPIES
 LOADS = 4
 BLOCK = 128
 SORT_PAIRS = 4
-CHUNK = 16
+CHUNK = 8
+AHEAD = 5
 GROUP = 8
-QUAD = 4
+PAIR = 2
 HALF = V // 2
 K_ROWS = 4
 W_CHUNK = 32
@@ -87,7 +88,7 @@ def tile_gccgc_pa_t_kernel(tc, x_pad, rel, A, w3, b3, out):
             raw_pool = first.enter_context(tc.tile_pool(name="raw", bufs=4))
             row_pool = first.enter_context(tc.tile_pool(name="row", bufs=1))
             sort_pool = first.enter_context(tc.tile_pool(name="sort", bufs=2))
-            win_pool = first.enter_context(tc.tile_pool(name="win", bufs=3))
+            win_pool = first.enter_context(tc.tile_pool(name="win", bufs=6))
             odd_pool = first.enter_context(tc.tile_pool(name="odd", bufs=3))
             sum_pool = first.enter_context(tc.tile_pool(name="sum", bufs=2))
             win_pool_w = first.enter_context(tc.tile_pool(name="w_in", bufs=1))
@@ -193,32 +194,30 @@ def tile_gccgc_pa_t_kernel(tc, x_pad, rel, A, w3, b3, out):
             def multiply(group):
                 x_codes, x_scales = x_mx_of[group]
                 key = group * GROUP // W_CHUNK
-                for quad in range(GROUP // QUAD):
-                    q0 = group * GROUP % W_CHUNK + quad * QUAD
-                    w_cols = slice(q0 * V, (q0 + QUAD) * V)
-                    acc = acc_psum.tile([P, QUAD * QUAD * V], F32, tag="acc", name="acc")
-                    acc_of[(group, quad)] = acc
-                    for q in range(QUAD):
-                        t_cols = slice((quad * QUAD + q) * T, (quad * QUAD + q + 1) * T)
-                        nc.tensor.matmul_mx(
-                            out=acc[:, q * QUAD * V : (q + 1) * QUAD * V],
-                            lhsT=x_codes[:, t_cols].bitcast(FP8X4),
-                            lhsT_scale=x_scales[:, t_cols],
-                            rhs=w_codes_of[key][:, w_cols].bitcast(FP8X4),
-                            rhs_scale=w_scales_of[key][:, w_cols],
-                            start=True,
-                            stop=True,
-                        )
+                acc = acc_psum.tile([P, GROUP * PAIR * V], F32, tag="acc", name="acc")
+                acc_of[group] = acc
+                for c in range(GROUP):
+                    first_w = (group * GROUP % W_CHUNK + c // PAIR * PAIR) * V
+                    w_cols = slice(first_w, first_w + PAIR * V)
+                    t_cols = slice(c * T, (c + 1) * T)
+                    nc.tensor.matmul_mx(
+                        out=acc[:, c * PAIR * V : (c + 1) * PAIR * V],
+                        lhsT=x_codes[:, t_cols].bitcast(FP8X4),
+                        lhsT_scale=x_scales[:, t_cols],
+                        rhs=w_codes_of[key][:, w_cols].bitcast(FP8X4),
+                        rhs_scale=w_scales_of[key][:, w_cols],
+                        start=True,
+                        stop=True,
+                    )
 
             def collect(group):
                 block = group // groups_in_block
                 if group % groups_in_block == 0:
                     z_sb_of[block] = z_pool.tile([P, BLOCK, V], BF16, name="z_sb")
-                for quad in range(GROUP // QUAD):
-                    c0 = group % groups_in_block * GROUP + quad * QUAD
-                    own = acc_of[(group, quad)][:].rearrange("p (blk i) -> p blk i", i=V)[:, 0 : QUAD * QUAD : QUAD + 1, :]
-                    dst = z_sb_of[block][:, c0 : c0 + QUAD, :]
-                    nc.scalar.copy(out=dst, in_=own)
+                c0 = group % groups_in_block * GROUP
+                own = acc_of[group][:].rearrange("p (h b i) -> p h b i", b=2 * PAIR, i=V)[:, :, 0 : 2 * PAIR : 2 * PAIR - 1, :]
+                dst = z_sb_of[block][:, c0 : c0 + GROUP, :].rearrange("p (h o) i -> p h o i", o=PAIR)
+                nc.scalar.copy(out=dst, in_=own)
 
             def turn(block, quarter):
                 z_words = z_sb_of[block][:].bitcast(F32)
@@ -228,10 +227,12 @@ def tile_gccgc_pa_t_kernel(tc, x_pad, rel, A, w3, b3, out):
                     nc.tensor.transpose(z_ps[:, i, :], z_words[:, :, 4 * quarter + i], unsort[:])
 
             def spread(block, quarter):
-                nc.scalar.copy(
-                    out=z_t[:, block].bitcast(F32)[:, :, 4 * quarter : 4 * quarter + 4],
-                    in_=z_ps_of[(block, quarter)][:].rearrange("p i t -> p t i"),
-                )
+                dst = z_t[:, block].bitcast(F32)[:, :, 4 * quarter : 4 * quarter + 4]
+                src = z_ps_of[(block, quarter)][:].rearrange("p i t -> p t i")
+                if block == n_blocks - 1 and quarter % 2 == 1:
+                    nc.vector.tensor_copy(out=dst, in_=src)
+                else:
+                    nc.scalar.copy(out=dst, in_=src)
 
             def load_mix():
                 mix["b3"] = raw_pool.tile([P, P], BF16, tag="raw", name="b3_in")
@@ -239,13 +240,50 @@ def tile_gccgc_pa_t_kernel(tc, x_pad, rel, A, w3, b3, out):
                 mix["w3"] = raw_pool.tile([P, OUT // P, C], BF16, tag="raw", name="w3_rows")
                 nc.sync.dma_start(out=mix["w3"][:], in_=w3.rearrange("(a p) c -> p a c", p=P))
 
+            def turn_mix(two):
+                w3_ps = tz_psum.tile([P, 2, 2, P], F32, tag="tz", name="w3_ps")
+                mix[two] = w3_ps
+                for a in range(2):
+                    for h in range(2):
+                        nc.tensor.transpose(
+                            w3_ps[:, a, h, :], mix["w3"][:, 2 * two + a, :].bitcast(F32)[:, h : C // 2 : 2], ident[:]
+                        )
+
+            def lay_mix(two):
+                if two == 0:
+                    mix["in"] = win_pool_w.tile([P, OUT, PACK], BF16, align_bytes=64, tag="w_in", name="w3_in")
+                nc.scalar.copy(
+                    out=mix["in"][:].bitcast(F32)[:, 2 * two * P : (2 * two + 2) * P, :].rearrange(
+                        "p (a o) h -> p a o h", a=2
+                    ),
+                    in_=mix[two][:].rearrange("p a h o -> p a o h"),
+                )
+
+            def quantise_mix():
+                nc.vector.quantize_mx(
+                    out=w3_codes[:].bitcast(FP8X4), scales=w3_scales[:], in_=mix["in"][:].rearrange("p o r -> p (o r)")
+                )
+
+            def turn_bias():
+                nc.vector.memset(b3_rows[:], 0.0)
+                nc.vector.tensor_copy(out=b3_rows[0 : OUT // P, :], in_=mix["b3"][0 : OUT // P, :])
+                mix["b3_ps"] = tz_psum.tile([P, P], F32, tag="tz", name="b3_ps")
+                nc.tensor.transpose(mix["b3_ps"][:], b3_rows[:], ident[:])
+
+            def spread_bias():
+                nc.vector.tensor_copy(out=b3_cols[:], in_=mix["b3_ps"][:, 0 : OUT // P])
+
             turning = {}
             for step in range((n_blocks - 1) * groups_in_block):
                 u = step % groups_in_block
-                if step < n_ip // 2:
-                    turning[step] = [2 * u - 8, 2 * u - 7] if u >= n_loads else []
+                start = n_loads if step < groups_in_block else 2
+                double = 5 if step < groups_in_block else 3
+                if u < start:
+                    turning[step] = []
+                elif u < start + double:
+                    turning[step] = [2 * (u - start), 2 * (u - start) + 1]
                 else:
-                    turning[step] = [u]
+                    turning[step] = [u + 1] if u + 1 < n_ip else []
 
             def turn_mix(two):
                 w3_ps = tz_psum.tile([P, 2, 2, P], F32, tag="tz", name="w3_ps")
@@ -285,6 +323,8 @@ def tile_gccgc_pa_t_kernel(tc, x_pad, rel, A, w3, b3, out):
                 u = step % groups_in_block
                 if step < n_ip // 2:
                     turning[step] = [2 * u - 8, 2 * u - 7] if u >= n_loads else []
+                elif u < n_loads:
+                    turning[step] = [2 * u - 4, 2 * u - 3] if u >= 2 else []
                 else:
                     turning[step] = [u]
 
@@ -294,8 +334,8 @@ def tile_gccgc_pa_t_kernel(tc, x_pad, rel, A, w3, b3, out):
             sort_block(0, range(PAIRS // SORT_PAIRS))
             for part in range(1, n_loads):
                 load_rel(0, part)
-            load_frames(0)
-            load_frames(1)
+            for chunk in range(AHEAD):
+                load_frames(chunk)
             nc.vector.tensor_copy(
                 out=unsort[:].rearrange("p (w s) -> p s w", s=2), in_=ident[:].rearrange("p (s w) -> p s w", s=2)
             )
@@ -313,16 +353,18 @@ def tile_gccgc_pa_t_kernel(tc, x_pad, rel, A, w3, b3, out):
             odd_windows(0)
             odd_windows(1)
 
-            for s in range(n_groups + 4):
+            for s in range(n_groups + 5):
                 block, g = divmod(s, groups_in_block)
                 inside = s < n_groups
-                if s % groups_in_chunk == 0 and s // groups_in_chunk + 2 < n_chunks:
-                    load_frames(s // groups_in_chunk + 2)
+                if s % groups_in_chunk == 0 and s // groups_in_chunk + AHEAD < n_chunks:
+                    load_frames(s // groups_in_chunk + AHEAD)
+                if s + 2 < n_groups:
+                    odd_windows(s + 2)
                 if s >= 1:
                     for ip in turning.get(s - 1, []):
                         lay_weights((s - 1) // groups_in_block + 1, ip, False)
-                if s + 2 < n_groups:
-                    odd_windows(s + 2)
+                for ip in turning.get(s, []):
+                    turn_weights(block + 1, ip)
                 if inside:
                     quantise_windows(s)
                     if g < 2:
@@ -340,15 +382,13 @@ def tile_gccgc_pa_t_kernel(tc, x_pad, rel, A, w3, b3, out):
                         load_rel(block + 2, g // 2)
                 if block + 2 < n_blocks and g >= 2 * n_loads and g % 2 == 0:
                     add_static(block + 2, 0, g // 2 - n_loads)
-                if 1 <= s <= n_groups:
-                    collect(s - 1)
-                for ip in turning.get(s, []):
-                    turn_weights(block + 1, ip)
+                if 2 <= s < n_groups + 2:
+                    collect(s - 2)
+                if block > 0 and 3 <= g < 5:
+                    for quarter in range(2 * g - 6, 2 * g - 4):
+                        spread(block - 1, quarter)
                 if block > 0 and 2 <= g < 4:
                     for quarter in range(2 * g - 4, 2 * g - 2):
-                        spread(block - 1, quarter)
-                if block > 0 and 1 <= g < 3:
-                    for quarter in range(2 * g - 2, 2 * g):
                         turn(block - 1, quarter)
                 if g == 1 and block + 1 < n_blocks:
                     load_block(block + 1)

@@ -28,8 +28,7 @@ SHIFT = TAPS // COPIES
 LOADS = 4
 BLOCK = 128
 SORT_PAIRS = 4
-CHUNK = 8
-AHEAD = 5
+AHEAD = 4
 GROUP = 8
 PAIR = 2
 HALF = V // 2
@@ -42,13 +41,11 @@ T_STEP = N_TILE // V
 def tile_gccgc_pa_t_kernel(tc, x_pad, rel, A, w3, b3, out):
     nc = tc.nc
     n_groups = C // GROUP
-    n_chunks = C // CHUNK
     n_blocks = C // BLOCK
-    groups_in_chunk = CHUNK // GROUP
     groups_in_block = BLOCK // GROUP
     n_loads = TAPS // K_ROWS
     n_ip = V // 2
-    run = (CHUNK - 1) * PITCH + T + 2
+    run = (GROUP - 1) * PITCH + T + 1
 
     out_words = out.rearrange("b o t i -> (b o t i)")
     scratch = out_words[0 : PAIRS * COPIES * C * PITCH].rearrange("(blk x) -> blk x", blk=n_blocks)
@@ -78,26 +75,28 @@ def tile_gccgc_pa_t_kernel(tc, x_pad, rel, A, w3, b3, out):
         make_identity(nc, ident[:])
         unsort = keep.tile([P, P], F32)
         a_all = keep.tile([P, V * V], BF16)
-        w3_codes = keep.tile([P, OUT], U32, align_bytes=64)
-        w3_scales = keep.tile([P, OUT], U8, align_bytes=64)
         b3_rows = keep.tile([P, P], F32)
         b3_cols = keep.tile([P, OUT // P], F32)
         z_t = keep.tile([P, PACK, T, V], BF16)
+
+        wq_pool = stack.enter_context(tc.tile_pool(name="wq", bufs=4))
 
         with ExitStack() as first:
             raw_pool = first.enter_context(tc.tile_pool(name="raw", bufs=4))
             row_pool = first.enter_context(tc.tile_pool(name="row", bufs=1))
             sort_pool = first.enter_context(tc.tile_pool(name="sort", bufs=2))
-            win_pool = first.enter_context(tc.tile_pool(name="win", bufs=6))
+            win_pool = first.enter_context(tc.tile_pool(name="win", bufs=7))
             odd_pool = first.enter_context(tc.tile_pool(name="odd", bufs=3))
             sum_pool = first.enter_context(tc.tile_pool(name="sum", bufs=2))
             win_pool_w = first.enter_context(tc.tile_pool(name="w_in", bufs=1))
-            wq_pool = first.enter_context(tc.tile_pool(name="wq", bufs=4))
             xq_pool = first.enter_context(tc.tile_pool(name="xq", bufs=2))
             z_pool = first.enter_context(tc.tile_pool(name="z", bufs=2))
             acc_psum = first.enter_context(tc.psum_pool(name="acc", bufs=3))
             tw_psum = first.enter_context(tc.psum_pool(name="tw", bufs=3))
             tz_psum = first.enter_context(tc.psum_pool(name="tz", bufs=2))
+
+            def odd_loaded(group):
+                return group % 4 == 3
 
             def load_block(block):
                 x_rows_of[block] = row_pool.tile([P, FRAMES * V], BF16, name="x_rows")
@@ -116,12 +115,14 @@ def tile_gccgc_pa_t_kernel(tc, x_pad, rel, A, w3, b3, out):
                             out=both[s, :, j0 : j0 + SORT_PAIRS, :], in_=rows[:, :, SHIFT * s : SHIFT * s + PITCH]
                         )
 
-            def load_frames(chunk):
-                frames_of[chunk] = win_pool.tile([P, CHUNK * PITCH], F32, align_bytes=64, name="frames")
-                rows = scratch[chunk * CHUNK // BLOCK].rearrange("(row x) -> row x", row=PAIRS * COPIES)
-                for lo in range(LOADS):
-                    w0 = (chunk * CHUNK % BLOCK) * PITCH + 2 * lo
-                    nc.sync.dma_start(out=frames_of[chunk][lo:P:LOADS, 0:run], in_=rows[:, w0 : w0 + run])
+            def load_frames(group):
+                rows = scratch[group // groups_in_block].rearrange("(row x) -> row x", row=PAIRS * COPIES)
+                for odd in range(2 if odd_loaded(group) else 1):
+                    frames = win_pool.tile([P, GROUP * PITCH], F32, align_bytes=64, tag="frames", name="frames")
+                    frames_of[(group, odd)] = frames
+                    for lo in range(LOADS):
+                        w0 = group % groups_in_block * GROUP * PITCH + 2 * lo + odd
+                        nc.sync.dma_start(out=frames[lo:P:LOADS, 0:run], in_=rows[:, w0 : w0 + run])
 
             def load_rel(block, part):
                 raw = raw_pool.tile([P, K_ROWS, V * V], BF16, tag="raw", name="raw")
@@ -163,8 +164,8 @@ def tile_gccgc_pa_t_kernel(tc, x_pad, rel, A, w3, b3, out):
 
             def quantise_weights(block, part):
                 key = block * (BLOCK // W_CHUNK) + part
-                w_codes_of[key] = wq_pool.tile([P, W_CHUNK * V], U32, align_bytes=64, name="w_codes")
-                w_scales_of[key] = wq_pool.tile([P, W_CHUNK * V], U8, align_bytes=64, name="w_scales")
+                w_codes_of[key] = wq_pool.tile([P, W_CHUNK * V], U32, align_bytes=64, tag="w_codes", name="w_codes")
+                w_scales_of[key] = wq_pool.tile([P, W_CHUNK * V], U8, align_bytes=64, tag="w_scales", name="w_scales")
                 nc.vector.quantize_mx(
                     out=w_codes_of[key][:].bitcast(FP8X4),
                     scales=w_scales_of[key][:],
@@ -172,21 +173,23 @@ def tile_gccgc_pa_t_kernel(tc, x_pad, rel, A, w3, b3, out):
                 )
 
             def odd_windows(group):
-                c0 = group % groups_in_chunk * GROUP
+                if odd_loaded(group):
+                    return
                 odd_of[group] = odd_pool.tile([P, GROUP, T], F32, align_bytes=64, name="odd")
-                src = frames_of[group // groups_in_chunk][:].rearrange("p (c f) -> p c f", c=CHUNK)
-                nc.scalar.copy(out=odd_of[group][:], in_=src[:, c0 : c0 + GROUP, 1 : T + 1])
+                src = frames_of[(group, 0)][:].rearrange("p (c f) -> p c f", c=GROUP)
+                nc.scalar.copy(out=odd_of[group][:], in_=src[:, :, 1 : T + 1])
 
             def quantise_windows(group):
                 x_codes = xq_pool.tile([P, GROUP * T], U32, align_bytes=64, name="x_codes")
                 x_scales = xq_pool.tile([P, GROUP * T], U8, align_bytes=64, name="x_scales")
                 x_mx_of[group] = (x_codes, x_scales)
-                frames = frames_of[group // groups_in_chunk]
                 for c in range(GROUP):
-                    f0 = (group % groups_in_chunk * GROUP + c) * PITCH
                     for odd in range(2):
                         cols = slice(c * T + odd * T // 2, c * T + (odd + 1) * T // 2)
-                        src = odd_of[group][:, c, :] if odd else frames[:, f0 : f0 + T]
+                        if odd and not odd_loaded(group):
+                            src = odd_of[group][:, c, :]
+                        else:
+                            src = frames_of[(group, odd)][:, c * PITCH : c * PITCH + T]
                         nc.vector.quantize_mx(
                             out=x_codes[:, cols].bitcast(FP8X4), scales=x_scales[:, cols], in_=src.bitcast(BF16)
                         )
@@ -260,8 +263,10 @@ def tile_gccgc_pa_t_kernel(tc, x_pad, rel, A, w3, b3, out):
                 )
 
             def quantise_mix():
+                mix["codes"] = wq_pool.tile([P, OUT], U32, align_bytes=64, tag="w_codes", name="w3_codes")
+                mix["scales"] = wq_pool.tile([P, OUT], U8, align_bytes=64, tag="w_scales", name="w3_scales")
                 nc.vector.quantize_mx(
-                    out=w3_codes[:].bitcast(FP8X4), scales=w3_scales[:], in_=mix["in"][:].rearrange("p o r -> p (o r)")
+                    out=mix["codes"][:].bitcast(FP8X4), scales=mix["scales"][:], in_=mix["in"][:].rearrange("p o r -> p (o r)")
                 )
 
             def turn_bias():
@@ -276,8 +281,8 @@ def tile_gccgc_pa_t_kernel(tc, x_pad, rel, A, w3, b3, out):
             turning = {}
             for step in range((n_blocks - 1) * groups_in_block):
                 u = step % groups_in_block
-                start = n_loads if step < groups_in_block else 2
-                double = 5 if step < groups_in_block else 3
+                start = 2 + n_loads if step < groups_in_block else 2
+                double = 7 if step < groups_in_block else 3
                 if u < start:
                     turning[step] = []
                 elif u < start + double:
@@ -285,68 +290,23 @@ def tile_gccgc_pa_t_kernel(tc, x_pad, rel, A, w3, b3, out):
                 else:
                     turning[step] = [u + 1] if u + 1 < n_ip else []
 
-            def turn_mix(two):
-                w3_ps = tz_psum.tile([P, 2, 2, P], F32, tag="tz", name="w3_ps")
-                mix[two] = w3_ps
-                for a in range(2):
-                    for h in range(2):
-                        nc.tensor.transpose(
-                            w3_ps[:, a, h, :], mix["w3"][:, 2 * two + a, :].bitcast(F32)[:, h : C // 2 : 2], ident[:]
-                        )
-
-            def lay_mix(two):
-                if two == 0:
-                    mix["in"] = win_pool_w.tile([P, OUT, PACK], BF16, align_bytes=64, tag="w_in", name="w3_in")
-                nc.scalar.copy(
-                    out=mix["in"][:].bitcast(F32)[:, 2 * two * P : (2 * two + 2) * P, :].rearrange(
-                        "p (a o) h -> p a o h", a=2
-                    ),
-                    in_=mix[two][:].rearrange("p a h o -> p a o h"),
-                )
-
-            def quantise_mix():
-                nc.vector.quantize_mx(
-                    out=w3_codes[:].bitcast(FP8X4), scales=w3_scales[:], in_=mix["in"][:].rearrange("p o r -> p (o r)")
-                )
-
-            def turn_bias():
-                nc.vector.memset(b3_rows[:], 0.0)
-                nc.vector.tensor_copy(out=b3_rows[0 : OUT // P, :], in_=mix["b3"][0 : OUT // P, :])
-                mix["b3_ps"] = tz_psum.tile([P, P], F32, tag="tz", name="b3_ps")
-                nc.tensor.transpose(mix["b3_ps"][:], b3_rows[:], ident[:])
-
-            def spread_bias():
-                nc.vector.tensor_copy(out=b3_cols[:], in_=mix["b3_ps"][:, 0 : OUT // P])
-
-            turning = {}
-            for step in range((n_blocks - 1) * groups_in_block):
-                u = step % groups_in_block
-                if step < n_ip // 2:
-                    turning[step] = [2 * u - 8, 2 * u - 7] if u >= n_loads else []
-                elif u < n_loads:
-                    turning[step] = [2 * u - 4, 2 * u - 3] if u >= 2 else []
-                else:
-                    turning[step] = [u]
-
-            load_block(0)
             nc.sync.dma_start(out=a_all[:], in_=A.rearrange("j i -> (j i)").partition_broadcast(P))
-            load_rel(0, 0)
-            sort_block(0, range(PAIRS // SORT_PAIRS))
-            for part in range(1, n_loads):
+            for part in range(n_loads):
                 load_rel(0, part)
-            for chunk in range(AHEAD):
-                load_frames(chunk)
+            load_block(0)
             nc.vector.tensor_copy(
                 out=unsort[:].rearrange("p (w s) -> p s w", s=2), in_=ident[:].rearrange("p (s w) -> p s w", s=2)
             )
-            for half in range(2):
-                for part in range(n_loads):
-                    add_static(0, half, part)
-                    if half == 1:
-                        load_rel(1, part)
-                        for ip in range(2 * part, 2 * part + 2):
-                            turn_weights(0, ip)
-                            lay_weights(0, ip, ip % 2 == 1)
+            for part in range(n_loads):
+                add_static(0, 0, part)
+            for part in range(n_loads):
+                sort_block(0, [part])
+                add_static(0, 1, part)
+                for ip in range(2 * part, 2 * part + 2):
+                    turn_weights(0, ip)
+                    lay_weights(0, ip, False)
+            for group in range(AHEAD):
+                load_frames(group)
             for ip in range(n_ip // 2, n_ip):
                 turn_weights(0, ip)
                 lay_weights(0, ip, ip % 2 == 1)
@@ -356,8 +316,10 @@ def tile_gccgc_pa_t_kernel(tc, x_pad, rel, A, w3, b3, out):
             for s in range(n_groups + 5):
                 block, g = divmod(s, groups_in_block)
                 inside = s < n_groups
-                if s % groups_in_chunk == 0 and s // groups_in_chunk + AHEAD < n_chunks:
-                    load_frames(s // groups_in_chunk + AHEAD)
+                if s + AHEAD < n_groups:
+                    load_frames(s + AHEAD)
+                if s < n_loads:
+                    load_rel(1, s)
                 if s + 2 < n_groups:
                     odd_windows(s + 2)
                 if s >= 1:
@@ -371,16 +333,18 @@ def tile_gccgc_pa_t_kernel(tc, x_pad, rel, A, w3, b3, out):
                         for part in range(2 * g, 2 * g + 2):
                             quantise_weights(block, part)
                     multiply(s)
-                if block == 0 and g < n_loads:
-                    add_static(1, 0, g)
-                if block == 0 and n_loads <= g < 2 * n_loads:
-                    add_static(1, 1, g - n_loads)
-                    load_rel(2, g - n_loads)
+                if block == 0 and 2 <= g < 2 + n_loads:
+                    add_static(1, 0, g - 2)
+                if block == 0 and 2 + n_loads <= g < 2 + 2 * n_loads:
+                    add_static(1, 1, g - 2 - n_loads)
+                    load_rel(2, g - 2 - n_loads)
+                if block == 0 and 2 + 2 * n_loads <= g < 2 + 3 * n_loads:
+                    add_static(2, 0, g - 2 - 2 * n_loads)
                 if block > 0 and block + 1 < n_blocks and g < 2 * n_loads and g % 2 == 0:
                     add_static(block + 1, 1, g // 2)
                     if block + 2 < n_blocks:
                         load_rel(block + 2, g // 2)
-                if block + 2 < n_blocks and g >= 2 * n_loads and g % 2 == 0:
+                if block > 0 and block + 2 < n_blocks and g >= 2 * n_loads and g % 2 == 0:
                     add_static(block + 2, 0, g // 2 - n_loads)
                 if 2 <= s < n_groups + 2:
                     collect(s - 2)
@@ -436,8 +400,8 @@ def tile_gccgc_pa_t_kernel(tc, x_pad, rel, A, w3, b3, out):
                 y_ps = y_psum.tile([P, N_TILE], F32, tag="y_ps")
                 nc.tensor.matmul_mx(
                     out=y_ps[:],
-                    lhsT=w3_codes[:, o_cols].bitcast(FP8X4),
-                    lhsT_scale=w3_scales[:, o_cols],
+                    lhsT=mix["codes"][:, o_cols].bitcast(FP8X4),
+                    lhsT_scale=mix["scales"][:, o_cols],
                     rhs=z_codes_of[step][:].bitcast(FP8X4),
                     rhs_scale=z_scales_of[step][:],
                     start=True,

@@ -28,7 +28,8 @@ SHIFT = TAPS // COPIES
 LOADS = 4
 BLOCK = 128
 SORT_PAIRS = 4
-AHEAD = 4
+AHEAD = 2
+CHUNK = 16
 GROUP = 8
 PAIR = 2
 HALF = V // 2
@@ -42,10 +43,12 @@ def tile_gccgc_pa_t_kernel(tc, x_pad, rel, A, w3, b3, out):
     nc = tc.nc
     n_groups = C // GROUP
     n_blocks = C // BLOCK
+    n_chunks = C // CHUNK
+    groups_in_chunk = CHUNK // GROUP
     groups_in_block = BLOCK // GROUP
     n_loads = TAPS // K_ROWS
     n_ip = V // 2
-    run = (GROUP - 1) * PITCH + T + 1
+    run = (CHUNK - 1) * PITCH + T + 1
 
     out_words = out.rearrange("b o t i -> (b o t i)")
     scratch = out_words[0 : PAIRS * COPIES * C * PITCH].rearrange("(blk x) -> blk x", blk=n_blocks)
@@ -85,18 +88,18 @@ def tile_gccgc_pa_t_kernel(tc, x_pad, rel, A, w3, b3, out):
             raw_pool = first.enter_context(tc.tile_pool(name="raw", bufs=4))
             row_pool = first.enter_context(tc.tile_pool(name="row", bufs=1))
             sort_pool = first.enter_context(tc.tile_pool(name="sort", bufs=2))
-            win_pool = first.enter_context(tc.tile_pool(name="win", bufs=7))
+            win_pool = first.enter_context(tc.tile_pool(name="win", bufs=3))
             odd_pool = first.enter_context(tc.tile_pool(name="odd", bufs=3))
             sum_pool = first.enter_context(tc.tile_pool(name="sum", bufs=2))
             win_pool_w = first.enter_context(tc.tile_pool(name="w_in", bufs=1))
-            xq_pool = first.enter_context(tc.tile_pool(name="xq", bufs=2))
+            xq_pool = first.enter_context(tc.tile_pool(name="xq", bufs=3))
             z_pool = first.enter_context(tc.tile_pool(name="z", bufs=2))
             acc_psum = first.enter_context(tc.psum_pool(name="acc", bufs=3))
             tw_psum = first.enter_context(tc.psum_pool(name="tw", bufs=3))
             tz_psum = first.enter_context(tc.psum_pool(name="tz", bufs=2))
 
-            def odd_loaded(group):
-                return group % 4 == 3
+            def odd_on_vector(group):
+                return group % 8 == 7
 
             def load_block(block):
                 x_rows_of[block] = row_pool.tile([P, FRAMES * V], BF16, name="x_rows")
@@ -115,14 +118,12 @@ def tile_gccgc_pa_t_kernel(tc, x_pad, rel, A, w3, b3, out):
                             out=both[s, :, j0 : j0 + SORT_PAIRS, :], in_=rows[:, :, SHIFT * s : SHIFT * s + PITCH]
                         )
 
-            def load_frames(group):
-                rows = scratch[group // groups_in_block].rearrange("(row x) -> row x", row=PAIRS * COPIES)
-                for odd in range(2 if odd_loaded(group) else 1):
-                    frames = win_pool.tile([P, GROUP * PITCH], F32, align_bytes=64, tag="frames", name="frames")
-                    frames_of[(group, odd)] = frames
-                    for lo in range(LOADS):
-                        w0 = group % groups_in_block * GROUP * PITCH + 2 * lo + odd
-                        nc.sync.dma_start(out=frames[lo:P:LOADS, 0:run], in_=rows[:, w0 : w0 + run])
+            def load_frames(chunk):
+                frames_of[chunk] = win_pool.tile([P, CHUNK * PITCH], F32, align_bytes=64, name="frames")
+                rows = scratch[chunk * CHUNK // BLOCK].rearrange("(row x) -> row x", row=PAIRS * COPIES)
+                for lo in range(LOADS):
+                    w0 = (chunk * CHUNK % BLOCK) * PITCH + 2 * lo
+                    nc.sync.dma_start(out=frames_of[chunk][lo:P:LOADS, 0:run], in_=rows[:, w0 : w0 + run])
 
             def load_rel(block, part):
                 raw = raw_pool.tile([P, K_ROWS, V * V], BF16, tag="raw", name="raw")
@@ -173,23 +174,25 @@ def tile_gccgc_pa_t_kernel(tc, x_pad, rel, A, w3, b3, out):
                 )
 
             def odd_windows(group):
-                if odd_loaded(group):
-                    return
+                c0 = group % groups_in_chunk * GROUP
                 odd_of[group] = odd_pool.tile([P, GROUP, T], F32, align_bytes=64, name="odd")
-                src = frames_of[(group, 0)][:].rearrange("p (c f) -> p c f", c=GROUP)
-                nc.scalar.copy(out=odd_of[group][:], in_=src[:, :, 1 : T + 1])
+                src = frames_of[group // groups_in_chunk][:].rearrange("p (c f) -> p c f", c=CHUNK)
+                src = src[:, c0 : c0 + GROUP, 1 : T + 1]
+                if odd_on_vector(group):
+                    nc.vector.tensor_copy(out=odd_of[group][:], in_=src)
+                else:
+                    nc.scalar.copy(out=odd_of[group][:], in_=src)
 
             def quantise_windows(group):
                 x_codes = xq_pool.tile([P, GROUP * T], U32, align_bytes=64, name="x_codes")
                 x_scales = xq_pool.tile([P, GROUP * T], U8, align_bytes=64, name="x_scales")
                 x_mx_of[group] = (x_codes, x_scales)
-                for c in range(GROUP):
-                    for odd in range(2):
+                frames = frames_of[group // groups_in_chunk]
+                for odd in range(2):
+                    for c in range(GROUP):
                         cols = slice(c * T + odd * T // 2, c * T + (odd + 1) * T // 2)
-                        if odd and not odd_loaded(group):
-                            src = odd_of[group][:, c, :]
-                        else:
-                            src = frames_of[(group, odd)][:, c * PITCH : c * PITCH + T]
+                        f0 = (group % groups_in_chunk * GROUP + c) * PITCH
+                        src = odd_of[group][:, c, :] if odd else frames[:, f0 : f0 + T]
                         nc.vector.quantize_mx(
                             out=x_codes[:, cols].bitcast(FP8X4), scales=x_scales[:, cols], in_=src.bitcast(BF16)
                         )
@@ -305,26 +308,27 @@ def tile_gccgc_pa_t_kernel(tc, x_pad, rel, A, w3, b3, out):
                 for ip in range(2 * part, 2 * part + 2):
                     turn_weights(0, ip)
                     lay_weights(0, ip, False)
-            for group in range(AHEAD):
-                load_frames(group)
+            for chunk in range(AHEAD):
+                load_frames(chunk)
             for ip in range(n_ip // 2, n_ip):
                 turn_weights(0, ip)
                 lay_weights(0, ip, ip % 2 == 1)
             odd_windows(0)
-            odd_windows(1)
 
             for s in range(n_groups + 5):
                 block, g = divmod(s, groups_in_block)
                 inside = s < n_groups
-                if s + AHEAD < n_groups:
-                    load_frames(s + AHEAD)
+                if s % groups_in_chunk == 0 and s // groups_in_chunk + AHEAD < n_chunks:
+                    load_frames(s // groups_in_chunk + AHEAD)
                 if s < n_loads:
                     load_rel(1, s)
-                if s + 2 < n_groups:
-                    odd_windows(s + 2)
+                if s + 1 < n_groups:
+                    odd_windows(s + 1)
                 if s >= 1:
                     for ip in turning.get(s - 1, []):
                         lay_weights((s - 1) // groups_in_block + 1, ip, False)
+                if 1 <= s <= n_groups:
+                    multiply(s - 1)
                 for ip in turning.get(s, []):
                     turn_weights(block + 1, ip)
                 if inside:
@@ -332,7 +336,6 @@ def tile_gccgc_pa_t_kernel(tc, x_pad, rel, A, w3, b3, out):
                     if g < 2:
                         for part in range(2 * g, 2 * g + 2):
                             quantise_weights(block, part)
-                    multiply(s)
                 if block == 0 and 2 <= g < 2 + n_loads:
                     add_static(1, 0, g - 2)
                 if block == 0 and 2 + n_loads <= g < 2 + 2 * n_loads:

@@ -28,8 +28,8 @@ SHIFT = TAPS // COPIES
 LOADS = 4
 BLOCK = 128
 SORT_PAIRS = 4
-AHEAD = 2
-CHUNK = 16
+AHEAD = 5
+CHUNK = 8
 GROUP = 8
 PAIR = 2
 HALF = V // 2
@@ -88,7 +88,7 @@ def tile_gccgc_pa_t_kernel(tc, x_pad, rel, A, w3, b3, out):
             raw_pool = first.enter_context(tc.tile_pool(name="raw", bufs=4))
             row_pool = first.enter_context(tc.tile_pool(name="row", bufs=1))
             sort_pool = first.enter_context(tc.tile_pool(name="sort", bufs=2))
-            win_pool = first.enter_context(tc.tile_pool(name="win", bufs=3))
+            win_pool = first.enter_context(tc.tile_pool(name="win", bufs=6))
             odd_pool = first.enter_context(tc.tile_pool(name="odd", bufs=3))
             sum_pool = first.enter_context(tc.tile_pool(name="sum", bufs=2))
             win_pool_w = first.enter_context(tc.tile_pool(name="w_in", bufs=1))
@@ -99,7 +99,7 @@ def tile_gccgc_pa_t_kernel(tc, x_pad, rel, A, w3, b3, out):
             tz_psum = first.enter_context(tc.psum_pool(name="tz", bufs=2))
 
             def odd_on_vector(group):
-                return group % 8 == 7
+                return group % groups_in_block in (0, 10, 12, 14) and 16 <= group < 49
 
             def load_block(block):
                 x_rows_of[block] = row_pool.tile([P, FRAMES * V], BF16, name="x_rows")
@@ -284,14 +284,12 @@ def tile_gccgc_pa_t_kernel(tc, x_pad, rel, A, w3, b3, out):
             turning = {}
             for step in range((n_blocks - 1) * groups_in_block):
                 u = step % groups_in_block
-                start = 2 + n_loads if step < groups_in_block else 2
-                double = 7 if step < groups_in_block else 3
-                if u < start:
-                    turning[step] = []
-                elif u < start + double:
-                    turning[step] = [2 * (u - start), 2 * (u - start) + 1]
-                else:
-                    turning[step] = [u + 1] if u + 1 < n_ip else []
+                start = 2 + n_loads if step < groups_in_block else 3
+                twice = range(start, start + 7) if step < groups_in_block else range(2 * n_loads, groups_in_block - 1, 2)
+                turning[step] = []
+                if start <= u < groups_in_block - 1:
+                    done = sum(2 if v in twice else 1 for v in range(start, u))
+                    turning[step] = list(range(done, done + (2 if u in twice else 1)))
 
             nc.sync.dma_start(out=a_all[:], in_=A.rearrange("j i -> (j i)").partition_broadcast(P))
             for part in range(n_loads):
@@ -333,9 +331,8 @@ def tile_gccgc_pa_t_kernel(tc, x_pad, rel, A, w3, b3, out):
                     turn_weights(block + 1, ip)
                 if inside:
                     quantise_windows(s)
-                    if g < 2:
-                        for part in range(2 * g, 2 * g + 2):
-                            quantise_weights(block, part)
+                    if g < BLOCK // W_CHUNK:
+                        quantise_weights(block, g)
                 if block == 0 and 2 <= g < 2 + n_loads:
                     add_static(1, 0, g - 2)
                 if block == 0 and 2 + n_loads <= g < 2 + 2 * n_loads:
@@ -343,10 +340,10 @@ def tile_gccgc_pa_t_kernel(tc, x_pad, rel, A, w3, b3, out):
                     load_rel(2, g - 2 - n_loads)
                 if block == 0 and 2 + 2 * n_loads <= g < 2 + 3 * n_loads:
                     add_static(2, 0, g - 2 - 2 * n_loads)
-                if block > 0 and block + 1 < n_blocks and g < 2 * n_loads and g % 2 == 0:
-                    add_static(block + 1, 1, g // 2)
+                if block > 0 and block + 1 < n_blocks and n_loads <= g < 2 * n_loads:
+                    add_static(block + 1, 1, g - n_loads)
                     if block + 2 < n_blocks:
-                        load_rel(block + 2, g // 2)
+                        load_rel(block + 2, g - n_loads)
                 if block > 0 and block + 2 < n_blocks and g >= 2 * n_loads and g % 2 == 0:
                     add_static(block + 2, 0, g // 2 - n_loads)
                 if 2 <= s < n_groups + 2:

@@ -28,6 +28,9 @@ SHIFT = TAPS // COPIES
 LOADS = 4
 BLOCK = 128
 SORT_PAIRS = 4
+SECOND_STEPS = (4, 6, 8, 10)
+SORT_STEPS = (3, 5, 7, 9)
+FIRST_STEPS = (11, 12, 13, 14)
 AHEAD = 5
 CHUNK = 8
 GROUP = 8
@@ -99,7 +102,7 @@ def tile_gccgc_pa_t_kernel(tc, x_pad, rel, A, w3, b3, out):
             tz_psum = first.enter_context(tc.psum_pool(name="tz", bufs=2))
 
             def odd_on_vector(group):
-                return group % groups_in_block in (0, 10, 12, 14) and 16 <= group < 49
+                return group % groups_in_block in (0, 13, 14, 15) and 12 < group < 49
 
             def load_block(block):
                 x_rows_of[block] = row_pool.tile([P, FRAMES * V], BF16, name="x_rows")
@@ -285,7 +288,7 @@ def tile_gccgc_pa_t_kernel(tc, x_pad, rel, A, w3, b3, out):
             for step in range((n_blocks - 1) * groups_in_block):
                 u = step % groups_in_block
                 start = 2 + n_loads if step < groups_in_block else 3
-                twice = range(start, start + 7) if step < groups_in_block else range(2 * n_loads, groups_in_block - 1, 2)
+                twice = range(start, start + 7) if step < groups_in_block else range(start + n_ip // 2, groups_in_block - 1)
                 turning[step] = []
                 if start <= u < groups_in_block - 1:
                     done = sum(2 if v in twice else 1 for v in range(start, u))
@@ -340,12 +343,12 @@ def tile_gccgc_pa_t_kernel(tc, x_pad, rel, A, w3, b3, out):
                     load_rel(2, g - 2 - n_loads)
                 if block == 0 and 2 + 2 * n_loads <= g < 2 + 3 * n_loads:
                     add_static(2, 0, g - 2 - 2 * n_loads)
-                if block > 0 and block + 1 < n_blocks and n_loads <= g < 2 * n_loads:
-                    add_static(block + 1, 1, g - n_loads)
+                if block > 0 and block + 1 < n_blocks and g in SECOND_STEPS:
+                    add_static(block + 1, 1, SECOND_STEPS.index(g))
                     if block + 2 < n_blocks:
-                        load_rel(block + 2, g - n_loads)
-                if block > 0 and block + 2 < n_blocks and g >= 2 * n_loads and g % 2 == 0:
-                    add_static(block + 2, 0, g // 2 - n_loads)
+                        load_rel(block + 2, SECOND_STEPS.index(g))
+                if block > 0 and block + 2 < n_blocks and g in FIRST_STEPS:
+                    add_static(block + 2, 0, FIRST_STEPS.index(g))
                 if 2 <= s < n_groups + 2:
                     collect(s - 2)
                 if block > 0 and 3 <= g < 5:
@@ -354,10 +357,10 @@ def tile_gccgc_pa_t_kernel(tc, x_pad, rel, A, w3, b3, out):
                 if block > 0 and 2 <= g < 4:
                     for quarter in range(2 * g - 4, 2 * g - 2):
                         turn(block - 1, quarter)
-                if g == 1 and block + 1 < n_blocks:
+                if g == 0 and block + 1 < n_blocks:
                     load_block(block + 1)
-                if 4 <= g < 4 + PAIRS // SORT_PAIRS and block + 1 < n_blocks:
-                    sort_block(block + 1, [g - 4])
+                if g in SORT_STEPS and block + 1 < n_blocks:
+                    sort_block(block + 1, [SORT_STEPS.index(g)])
                 if block == n_blocks - 1:
                     if g == 0:
                         load_mix()

@@ -375,7 +375,7 @@ def tile_gccgc_pa_t_kernel(tc, x_pad, rel, A, w3, b3, out):
                         spread_bias()
 
         zq_pool = stack.enter_context(tc.tile_pool(name="zq", bufs=2))
-        y_pool = stack.enter_context(tc.tile_pool(name="y", bufs=8))
+        y_pool = stack.enter_context(tc.tile_pool(name="y", bufs=6))
         y_psum = stack.enter_context(tc.psum_pool(name="y_ps", bufs=6))
         z_codes_of = {}
         z_scales_of = {}
@@ -410,9 +410,14 @@ def tile_gccgc_pa_t_kernel(tc, x_pad, rel, A, w3, b3, out):
                     start=True,
                     stop=True,
                 )
-                y = y_pool.tile([P, N_TILE], F32)
+                if a % 2 == 0:
+                    y = y_pool.tile([P, 2, N_TILE], F32)
                 if a % 3 == 1:
-                    nc.vector.tensor_scalar_add(out=y[:], in0=y_ps[:], scalar1=b3_cols[:, a : a + 1])
+                    nc.vector.tensor_scalar_add(out=y[:, a % 2], in0=y_ps[:], scalar1=b3_cols[:, a : a + 1])
                 else:
-                    nc.scalar.activation(out=y[:], in_=y_ps[:], func=IDENTITY, bias=b3_cols[:, a : a + 1])
-                nc.sync.dma_start(out=out[0, o_cols, t_rows, :].rearrange("o t i -> o (t i)"), in_=y[:])
+                    nc.scalar.activation(out=y[:, a % 2], in_=y_ps[:], func=IDENTITY, bias=b3_cols[:, a : a + 1])
+                if a % 2 == 1:
+                    nc.sync.dma_start(
+                        out=out[0, (a - 1) * P : (a + 1) * P, t_rows, :].rearrange("(two p) t i -> p two (t i)", p=P),
+                        in_=y[:],
+                    )

@@ -178,7 +178,7 @@ def tile_gccgc_pa_t_kernel(tc, x_pad, rel, A, w3, b3, out):
 
             def odd_windows(group):
                 c0 = group % groups_in_chunk * GROUP
-                odd_of[group] = odd_pool.tile([P, GROUP, T], F32, align_bytes=64, name="odd")
+                odd_of[group] = odd_pool.tile([P, GROUP, T], F32, align_bytes=64, tag="odd", name="odd")
                 src = frames_of[group // groups_in_chunk][:].rearrange("p (c f) -> p c f", c=CHUNK)
                 src = src[:, c0 : c0 + GROUP, 1 : T + 1]
                 if odd_on_vector(group):
@@ -294,8 +294,18 @@ def tile_gccgc_pa_t_kernel(tc, x_pad, rel, A, w3, b3, out):
                     done = sum(2 if v in twice else 1 for v in range(start, u))
                     turning[step] = list(range(done, done + (2 if u in twice else 1)))
 
-            nc.sync.dma_start(out=a_all[:], in_=A.rearrange("j i -> (j i)").partition_broadcast(P))
-            for part in range(n_loads):
+            load_rel(0, 0)
+            a_row = odd_pool.tile([P, V * V], BF16, align_bytes=64, tag="odd", name="a_row")
+            nc.vector.memset(a_row[:], 0.0)
+            ones = keep.tile([P, P], BF16)
+            nc.vector.memset(ones[:], 1.0)
+            nc.sync.dma_start(out=a_row[0:1, :], in_=A.rearrange("(one j) i -> one (j i)", one=1))
+            for half in range(2):
+                a_cols = slice(half * V * V // 2, (half + 1) * V * V // 2)
+                a_ps = tw_psum.tile([P, V * V // 2], F32, tag="tw", name="a_ps")
+                nc.tensor.matmul(a_ps[:], lhsT=ones[:], rhs=a_row[:, a_cols], start=True, stop=True)
+                nc.scalar.copy(out=a_all[:, a_cols], in_=a_ps[:])
+            for part in range(1, n_loads):
                 load_rel(0, part)
             load_block(0)
             nc.vector.tensor_copy(

@@ -31,6 +31,7 @@ SORT_PAIRS = 4
 SECOND_STEPS = (4, 6, 8, 10)
 SORT_STEPS = (3, 5, 7, 9)
 FIRST_STEPS = (11, 12, 13, 14)
+EARLY = 2
 AHEAD = 5
 CHUNK = 8
 GROUP = 8
@@ -294,6 +295,7 @@ def tile_gccgc_pa_t_kernel(tc, x_pad, rel, A, w3, b3, out):
                     done = sum(2 if v in twice else 1 for v in range(start, u))
                     turning[step] = list(range(done, done + (2 if u in twice else 1)))
 
+            load_block(0)
             load_rel(0, 0)
             a_row = odd_pool.tile([P, V * V], BF16, align_bytes=64, tag="odd", name="a_row")
             nc.vector.memset(a_row[:], 0.0)
@@ -307,24 +309,26 @@ def tile_gccgc_pa_t_kernel(tc, x_pad, rel, A, w3, b3, out):
                 nc.scalar.copy(out=a_all[:, a_cols], in_=a_ps[:])
             for part in range(1, n_loads):
                 load_rel(0, part)
-            load_block(0)
+            sort_block(0, [0, 1])
             nc.vector.tensor_copy(
                 out=unsort[:].rearrange("p (w s) -> p s w", s=2), in_=ident[:].rearrange("p (s w) -> p s w", s=2)
             )
             for part in range(n_loads):
                 add_static(0, 0, part)
+            sort_block(0, [2, 3])
+            for chunk in range(AHEAD):
+                load_frames(chunk)
             for part in range(n_loads):
-                sort_block(0, [part])
                 add_static(0, 1, part)
                 for ip in range(2 * part, 2 * part + 2):
                     turn_weights(0, ip)
                     lay_weights(0, ip, False)
-            for chunk in range(AHEAD):
-                load_frames(chunk)
             for ip in range(n_ip // 2, n_ip):
                 turn_weights(0, ip)
                 lay_weights(0, ip, ip % 2 == 1)
-            odd_windows(0)
+                if ip in [13,15]:
+                    odd_windows([13,15].index(ip))
+                    quantise_windows([13,15].index(ip))
 
             for s in range(n_groups + 5):
                 block, g = divmod(s, groups_in_block)
@@ -333,7 +337,7 @@ def tile_gccgc_pa_t_kernel(tc, x_pad, rel, A, w3, b3, out):
                     load_frames(s // groups_in_chunk + AHEAD)
                 if s < n_loads:
                     load_rel(1, s)
-                if s + 1 < n_groups:
+                if max(s + 1, EARLY) < n_groups and s + 1 >= EARLY:
                     odd_windows(s + 1)
                 if s >= 1:
                     for ip in turning.get(s - 1, []):
@@ -342,8 +346,9 @@ def tile_gccgc_pa_t_kernel(tc, x_pad, rel, A, w3, b3, out):
                     multiply(s - 1)
                 for ip in turning.get(s, []):
                     turn_weights(block + 1, ip)
-                if inside:
+                if EARLY <= s < n_groups:
                     quantise_windows(s)
+                if inside:
                     if g < BLOCK // W_CHUNK:
                         quantise_weights(block, g)
                 if block == 0 and 2 <= g < 2 + n_loads:

@@ -29,7 +29,7 @@ LOADS = 4
 BLOCK = 128
 SORT_PAIRS = 4
 SECOND_STEPS = (4, 6, 8, 10)
-SORT_STEPS = (3, 5, 7, 9)
+SORT_STEPS = (2, 3, 5, 7)
 FIRST_STEPS = (11, 12, 13, 14)
 EARLY = 2
 AHEAD = 5
@@ -64,6 +64,7 @@ def tile_gccgc_pa_t_kernel(tc, x_pad, rel, A, w3, b3, out):
         keep = stack.enter_context(tc.tile_pool(name="keep", bufs=1))
 
         x_rows_of = {}
+        rows_of = {}
         frames_of = {}
         raw_of = {}
         wsum_of = {}
@@ -103,24 +104,28 @@ def tile_gccgc_pa_t_kernel(tc, x_pad, rel, A, w3, b3, out):
             tz_psum = first.enter_context(tc.psum_pool(name="tz", bufs=2))
 
             def odd_on_vector(group):
-                return group % groups_in_block in (0, 13, 14, 15) and 12 < group < 49
+                return (group % groups_in_block in (0, 13, 14, 15) and 12 < group < 49) or 41 <= group < 49
 
             def load_block(block):
                 x_rows_of[block] = row_pool.tile([P, FRAMES * V], BF16, name="x_rows")
                 nc.sync.dma_start(out=x_rows_of[block][:], in_=x_blocks[block])
 
             def sort_block(block, parts):
-                both = scratch[block].rearrange("(jp s c f) -> s c jp f", jp=PAIRS, s=COPIES, c=BLOCK)
                 words = x_rows_of[block][:].bitcast(F32).rearrange("c (f jp) -> c jp f", jp=PAIRS)
                 for part in parts:
                     j0 = part * SORT_PAIRS
                     rows = sort_pool.tile([P, SORT_PAIRS, PITCH + SHIFT], F32, name="rows")
                     nc.vector.memset(rows[:, :, FRAMES : PITCH + SHIFT], 0.0)
                     nc.vector.tensor_copy(out=rows[:, :, 0:FRAMES], in_=words[:, j0 : j0 + SORT_PAIRS, :])
+                    rows_of[(block, part)] = rows
+
+            def store_sorted(block, parts):
+                both = scratch[block].rearrange("(jp s c f) -> s c jp f", jp=PAIRS, s=COPIES, c=BLOCK)
+                for part in parts:
+                    pairs = slice(part * SORT_PAIRS, (part + 1) * SORT_PAIRS)
+                    rows = rows_of[(block, part)]
                     for s in range(COPIES):
-                        nc.sync.dma_start(
-                            out=both[s, :, j0 : j0 + SORT_PAIRS, :], in_=rows[:, :, SHIFT * s : SHIFT * s + PITCH]
-                        )
+                        nc.sync.dma_start(out=both[s, :, pairs, :], in_=rows[:, :, SHIFT * s : SHIFT * s + PITCH])
 
             def load_frames(chunk):
                 frames_of[chunk] = win_pool.tile([P, CHUNK * PITCH], F32, align_bytes=64, name="frames")
@@ -310,12 +315,14 @@ def tile_gccgc_pa_t_kernel(tc, x_pad, rel, A, w3, b3, out):
             for part in range(1, n_loads):
                 load_rel(0, part)
             sort_block(0, [0, 1])
+            store_sorted(0, [0, 1])
             nc.vector.tensor_copy(
                 out=unsort[:].rearrange("p (w s) -> p s w", s=2), in_=ident[:].rearrange("p (s w) -> p s w", s=2)
             )
             for part in range(n_loads):
                 add_static(0, 0, part)
             sort_block(0, [2, 3])
+            store_sorted(0, [2, 3])
             for chunk in range(AHEAD):
                 load_frames(chunk)
             for part in range(n_loads):
@@ -337,6 +344,8 @@ def tile_gccgc_pa_t_kernel(tc, x_pad, rel, A, w3, b3, out):
                     load_frames(s // groups_in_chunk + AHEAD)
                 if s < n_loads:
                     load_rel(1, s)
+                if g - 1 in SORT_STEPS and block + 1 < n_blocks:
+                    store_sorted(block + 1, [SORT_STEPS.index(g - 1)])
                 if max(s + 1, EARLY) < n_groups and s + 1 >= EARLY:
                     odd_windows(s + 1)
                 if s >= 1:
@@ -360,8 +369,8 @@ def tile_gccgc_pa_t_kernel(tc, x_pad, rel, A, w3, b3, out):
                     add_static(2, 0, g - 2 - 2 * n_loads)
                 if block > 0 and block + 1 < n_blocks and g in SECOND_STEPS:
                     add_static(block + 1, 1, SECOND_STEPS.index(g))
-                    if block + 2 < n_blocks:
-                        load_rel(block + 2, SECOND_STEPS.index(g))
+                if block > 0 and block + 2 < n_blocks and g - 1 in SECOND_STEPS:
+                    load_rel(block + 2, SECOND_STEPS.index(g - 1))
                 if block > 0 and block + 2 < n_blocks and g in FIRST_STEPS:
                     add_static(block + 2, 0, FIRST_STEPS.index(g))
                 if 2 <= s < n_groups + 2:
@@ -372,8 +381,10 @@ def tile_gccgc_pa_t_kernel(tc, x_pad, rel, A, w3, b3, out):
                 if block > 0 and 2 <= g < 4:
                     for quarter in range(2 * g - 4, 2 * g - 2):
                         turn(block - 1, quarter)
-                if g == 0 and block + 1 < n_blocks:
-                    load_block(block + 1)
+                if s == 0:
+                    load_block(1)
+                if g == 12 and block + 2 < n_blocks:
+                    load_block(block + 2)
                 if g in SORT_STEPS and block + 1 < n_blocks:
                     sort_block(block + 1, [SORT_STEPS.index(g)])
                 if block == n_blocks - 1:

from contextlib import ExitStack

import concourse.mybir as mybir
from concourse.masks import make_identity

FLOPS = 2 * 512 * 128 * 512 * 32 + 2 * 1024 * 512 * 128 * 32

BF16 = mybir.dt.bfloat16
F32 = mybir.dt.float32
U32 = mybir.dt.uint32
U8 = mybir.dt.uint8
FP8X4 = mybir.dt.float8_e4m3fn_x4
ADD = mybir.AluOpType.add
IDENTITY = mybir.ActivationFunctionType.Identity

P = 128
PACK = 4
C = 512
T = 128
V = 32
TAPS = 16
FRAMES = 143
OUT = 1024
PAIRS = V // 2
PITCH = 144
COPIES = 2
SHIFT = TAPS // COPIES
LOADS = 4
BLOCK = 128
SORT_PAIRS = 4
SECOND_STEPS = (4, 6, 8, 10)
SORT_STEPS = (2, 3, 5, 7)
FIRST_STEPS = (11, 12, 13, 14)
EARLY = 2
AHEAD = 5
CHUNK = 8
GROUP = 8
PAIR = 2
HALF = V // 2
K_ROWS = 4
W_CHUNK = 32
N_TILE = 512
T_STEP = N_TILE // V


def tile_gccgc_pa_t_kernel(tc, x_pad, rel, A, w3, b3, out):
    nc = tc.nc
    n_groups = C // GROUP
    n_blocks = C // BLOCK
    n_chunks = C // CHUNK
    groups_in_chunk = CHUNK // GROUP
    groups_in_block = BLOCK // GROUP
    n_loads = TAPS // K_ROWS
    n_ip = V // 2
    run = (CHUNK - 1) * PITCH + T + 1

    out_words = out.rearrange("b o t i -> (b o t i)")
    scratch = out_words[0 : PAIRS * COPIES * C * PITCH].rearrange("(blk x) -> blk x", blk=n_blocks)
    rel_rows = rel[0].rearrange("(m r k) j i -> r m k (j i)", r=PACK, k=TAPS)
    x_blocks = x_pad[0].rearrange("(m r) f v -> r m (f v)", r=PACK)

    with ExitStack() as stack:
        stack.enter_context(tc.manual_schedule())
        keep = stack.enter_context(tc.tile_pool(name="keep", bufs=1))

        x_rows_of = {}
        rows_of = {}
        frames_of = {}
        raw_of = {}
        wsum_of = {}
        w_in_of = {}
        w_ps_of = {}
        w_codes_of = {}
        w_scales_of = {}
        odd_of = {}
        x_mx_of = {}
        acc_of = {}
        mix = {}
        z_sb_of = {}
        z_ps_of = {}

        ident = keep.tile([P, P], F32)
        make_identity(nc, ident[:])
        unsort = keep.tile([P, P], F32)
        a_all = keep.tile([P, V * V], BF16)
        b3_rows = keep.tile([P, P], F32)
        b3_cols = keep.tile([P, OUT // P], F32)
        z_t = keep.tile([P, PACK, T, V], BF16)

        wq_pool = stack.enter_context(tc.tile_pool(name="wq", bufs=4))

        with ExitStack() as first:
            raw_pool = first.enter_context(tc.tile_pool(name="raw", bufs=4))
            row_pool = first.enter_context(tc.tile_pool(name="row", bufs=1))
            sort_pool = first.enter_context(tc.tile_pool(name="sort", bufs=2))
            win_pool = first.enter_context(tc.tile_pool(name="win", bufs=6))
            odd_pool = first.enter_context(tc.tile_pool(name="odd", bufs=3))
            sum_pool = first.enter_context(tc.tile_pool(name="sum", bufs=2))
            win_pool_w = first.enter_context(tc.tile_pool(name="w_in", bufs=1))
            xq_pool = first.enter_context(tc.tile_pool(name="xq", bufs=3))
            z_pool = first.enter_context(tc.tile_pool(name="z", bufs=2))
            acc_psum = first.enter_context(tc.psum_pool(name="acc", bufs=3))
            tw_psum = first.enter_context(tc.psum_pool(name="tw", bufs=3))
            tz_psum = first.enter_context(tc.psum_pool(name="tz", bufs=2))

            def odd_on_vector(group):
                return (group % groups_in_block in (0, 13, 14, 15) and 12 < group < 49) or 41 <= group < 49

            def load_block(block):
                x_rows_of[block] = row_pool.tile([P, FRAMES * V], BF16, name="x_rows")
                nc.sync.dma_start(out=x_rows_of[block][:], in_=x_blocks[block])

            def sort_block(block, parts):
                words = x_rows_of[block][:].bitcast(F32).rearrange("c (f jp) -> c jp f", jp=PAIRS)
                for part in parts:
                    j0 = part * SORT_PAIRS
                    rows = sort_pool.tile([P, SORT_PAIRS, PITCH + SHIFT], F32, name="rows")
                    nc.vector.memset(rows[:, :, FRAMES : PITCH + SHIFT], 0.0)
                    nc.vector.tensor_copy(out=rows[:, :, 0:FRAMES], in_=words[:, j0 : j0 + SORT_PAIRS, :])
                    rows_of[(block, part)] = rows

            def store_sorted(block, parts):
                both = scratch[block].rearrange("(jp s c f) -> s c jp f", jp=PAIRS, s=COPIES, c=BLOCK)
                for part in parts:
                    pairs = slice(part * SORT_PAIRS, (part + 1) * SORT_PAIRS)
                    rows = rows_of[(block, part)]
                    for s in range(COPIES):
                        nc.sync.dma_start(out=both[s, :, pairs, :], in_=rows[:, :, SHIFT * s : SHIFT * s + PITCH])

            def load_frames(chunk):
                frames_of[chunk] = win_pool.tile([P, CHUNK * PITCH], F32, align_bytes=64, name="frames")
                rows = scratch[chunk * CHUNK // BLOCK].rearrange("(row x) -> row x", row=PAIRS * COPIES)
                for lo in range(LOADS):
                    w0 = (chunk * CHUNK % BLOCK) * PITCH + 2 * lo
                    nc.sync.dma_start(out=frames_of[chunk][lo:P:LOADS, 0:run], in_=rows[:, w0 : w0 + run])

            def load_rel(block, part):
                raw = raw_pool.tile([P, K_ROWS, V * V], BF16, tag="raw", name="raw")
                raw_of[(block, part)] = raw
                nc.sync.dma_start(out=raw[:], in_=rel_rows[block, :, part * K_ROWS : (part + 1) * K_ROWS, :])

            def add_static(block, half, part):
                if part == 0:
                    wsum_of[(block, half)] = sum_pool.tile([P, TAPS * V * HALF], BF16, name="wsum")
                sums = wsum_of[(block, half)][:].rearrange("c (jp k e i) -> c e k jp i", jp=PAIRS, k=TAPS, e=2)
                raw = raw_of[(block, part)][:].rearrange("c k (jp e i) -> c e k jp i", jp=PAIRS, e=2)
                static = a_all[:].rearrange("c (jp e i) -> c e jp i", jp=PAIRS, e=2)
                i_cols = slice(half * HALF, (half + 1) * HALF)
                for e in range(2):
                    nc.vector.tensor_tensor(
                        out=sums[:, e, part * K_ROWS : (part + 1) * K_ROWS],
                        in0=raw[:, e, :, :, i_cols],
                        in1=static[:, e, :, i_cols].unsqueeze(1).to_broadcast([P, K_ROWS, PAIRS, HALF]),
                        op=ADD,
                    )

            def turn_weights(block, ip):
                half, word = divmod(ip, HALF // 2)
                words = wsum_of[(block, half)][:].bitcast(F32).rearrange("c (p x) -> c p x", p=P)
                w_ps = tw_psum.tile([P, PACK, P], F32, tag="tw", name="w_ps")
                w_ps_of[(block, ip)] = w_ps
                for r in range(PACK):
                    nc.tensor.transpose(w_ps[:, r, :], words[:, :, r * HALF // 2 + word], ident[:])

            def lay_weights(block, ip, on_vector):
                if ip == 0:
                    w_in_of[block] = win_pool_w.tile([P, BLOCK, V, PACK], BF16, align_bytes=64, tag="w_in", name="w_in")
                src = w_ps_of[(block, ip)][:].bitcast(BF16).rearrange("p r (c h) -> p c h r", h=2)
                dst = w_in_of[block][:, :, 2 * ip : 2 * ip + 2, :]
                if on_vector:
                    nc.vector.tensor_copy(out=dst, in_=src)
                else:
                    nc.scalar.copy(out=dst, in_=src)

            def quantise_weights(block, part):
                key = block * (BLOCK // W_CHUNK) + part
                w_codes_of[key] = wq_pool.tile([P, W_CHUNK * V], U32, align_bytes=64, tag="w_codes", name="w_codes")
                w_scales_of[key] = wq_pool.tile([P, W_CHUNK * V], U8, align_bytes=64, tag="w_scales", name="w_scales")
                nc.vector.quantize_mx(
                    out=w_codes_of[key][:].bitcast(FP8X4),
                    scales=w_scales_of[key][:],
                    in_=w_in_of[block][:, part * W_CHUNK : (part + 1) * W_CHUNK].rearrange("p c i r -> p (c i r)"),
                )

            def odd_windows(group):
                c0 = group % groups_in_chunk * GROUP
                odd_of[group] = odd_pool.tile([P, GROUP, T], F32, align_bytes=64, tag="odd", name="odd")
                src = frames_of[group // groups_in_chunk][:].rearrange("p (c f) -> p c f", c=CHUNK)
                src = src[:, c0 : c0 + GROUP, 1 : T + 1]
                if odd_on_vector(group):
                    nc.vector.tensor_copy(out=odd_of[group][:], in_=src)
                else:
                    nc.scalar.copy(out=odd_of[group][:], in_=src)

            def quantise_windows(group):
                x_codes = xq_pool.tile([P, GROUP * T], U32, align_bytes=64, name="x_codes")
                x_scales = xq_pool.tile([P, GROUP * T], U8, align_bytes=64, name="x_scales")
                x_mx_of[group] = (x_codes, x_scales)
                frames = frames_of[group // groups_in_chunk]
                for odd in range(2):
                    for c in range(GROUP):
                        cols = slice(c * T + odd * T // 2, c * T + (odd + 1) * T // 2)
                        f0 = (group % groups_in_chunk * GROUP + c) * PITCH
                        src = odd_of[group][:, c, :] if odd else frames[:, f0 : f0 + T]
                        nc.vector.quantize_mx(
                            out=x_codes[:, cols].bitcast(FP8X4), scales=x_scales[:, cols], in_=src.bitcast(BF16)
                        )

            def multiply(group):
                x_codes, x_scales = x_mx_of[group]
                key = group * GROUP // W_CHUNK
                acc = acc_psum.tile([P, GROUP * PAIR * V], F32, tag="acc", name="acc")
                acc_of[group] = acc
                for c in range(GROUP):
                    first_w = (group * GROUP % W_CHUNK + c // PAIR * PAIR) * V
                    w_cols = slice(first_w, first_w + PAIR * V)
                    t_cols = slice(c * T, (c + 1) * T)
                    nc.tensor.matmul_mx(
                        out=acc[:, c * PAIR * V : (c + 1) * PAIR * V],
                        lhsT=x_codes[:, t_cols].bitcast(FP8X4),
                        lhsT_scale=x_scales[:, t_cols],
                        rhs=w_codes_of[key][:, w_cols].bitcast(FP8X4),
                        rhs_scale=w_scales_of[key][:, w_cols],
                        start=True,
                        stop=True,
                    )

            def collect(group):
                block = group // groups_in_block
                if group % groups_in_block == 0:
                    z_sb_of[block] = z_pool.tile([P, BLOCK, V], BF16, name="z_sb")
                c0 = group % groups_in_block * GROUP
                own = acc_of[group][:].rearrange("p (h b i) -> p h b i", b=2 * PAIR, i=V)[:, :, 0 : 2 * PAIR : 2 * PAIR - 1, :]
                dst = z_sb_of[block][:, c0 : c0 + GROUP, :].rearrange("p (h o) i -> p h o i", o=PAIR)
                nc.scalar.copy(out=dst, in_=own)

            def turn(block, quarter):
                z_words = z_sb_of[block][:].bitcast(F32)
                z_ps = tz_psum.tile([P, 4, T], F32, tag="tz", name="z_ps")
                z_ps_of[(block, quarter)] = z_ps
                for i in range(4):
                    nc.tensor.transpose(z_ps[:, i, :], z_words[:, :, 4 * quarter + i], unsort[:])

            def spread(block, quarter):
                dst = z_t[:, block].bitcast(F32)[:, :, 4 * quarter : 4 * quarter + 4]
                src = z_ps_of[(block, quarter)][:].rearrange("p i t -> p t i")
                if block == n_blocks - 1 and quarter % 2 == 1:
                    nc.vector.tensor_copy(out=dst, in_=src)
                else:
                    nc.scalar.copy(out=dst, in_=src)

            def load_mix():
                mix["b3"] = raw_pool.tile([P, P], BF16, tag="raw", name="b3_in")
                nc.sync.dma_start(out=mix["b3"][0 : OUT // P, :], in_=b3.rearrange("(a o) -> a o", o=P))
                mix["w3"] = raw_pool.tile([P, OUT // P, C], BF16, tag="raw", name="w3_rows")
                nc.sync.dma_start(out=mix["w3"][:], in_=w3.rearrange("(a p) c -> p a c", p=P))

            def turn_mix(two):
                w3_ps = tz_psum.tile([P, 2, 2, P], F32, tag="tz", name="w3_ps")
                mix[two] = w3_ps
                for a in range(2):
                    for h in range(2):
                        nc.tensor.transpose(
                            w3_ps[:, a, h, :], mix["w3"][:, 2 * two + a, :].bitcast(F32)[:, h : C // 2 : 2], ident[:]
                        )

            def lay_mix(two):
                if two == 0:
                    mix["in"] = win_pool_w.tile([P, OUT, PACK], BF16, align_bytes=64, tag="w_in", name="w3_in")
                nc.scalar.copy(
                    out=mix["in"][:].bitcast(F32)[:, 2 * two * P : (2 * two + 2) * P, :].rearrange(
                        "p (a o) h -> p a o h", a=2
                    ),
                    in_=mix[two][:].rearrange("p a h o -> p a o h"),
                )

            def quantise_mix():
                mix["codes"] = wq_pool.tile([P, OUT], U32, align_bytes=64, tag="w_codes", name="w3_codes")
                mix["scales"] = wq_pool.tile([P, OUT], U8, align_bytes=64, tag="w_scales", name="w3_scales")
                nc.vector.quantize_mx(
                    out=mix["codes"][:].bitcast(FP8X4), scales=mix["scales"][:], in_=mix["in"][:].rearrange("p o r -> p (o r)")
                )

            def turn_bias():
                nc.vector.memset(b3_rows[:], 0.0)
                nc.vector.tensor_copy(out=b3_rows[0 : OUT // P, :], in_=mix["b3"][0 : OUT // P, :])
                mix["b3_ps"] = tz_psum.tile([P, P], F32, tag="tz", name="b3_ps")
                nc.tensor.transpose(mix["b3_ps"][:], b3_rows[:], ident[:])

            def spread_bias():
                nc.vector.tensor_copy(out=b3_cols[:], in_=mix["b3_ps"][:, 0 : OUT // P])

            turning = {}
            for step in range((n_blocks - 1) * groups_in_block):
                u = step % groups_in_block
                start = 2 + n_loads if step < groups_in_block else 3
                twice = range(start, start + 7) if step < groups_in_block else range(start + n_ip // 2, groups_in_block - 1)
                turning[step] = []
                if start <= u < groups_in_block - 1:
                    done = sum(2 if v in twice else 1 for v in range(start, u))
                    turning[step] = list(range(done, done + (2 if u in twice else 1)))

            load_block(0)
            load_rel(0, 0)
            a_row = odd_pool.tile([P, V * V], BF16, align_bytes=64, tag="odd", name="a_row")
            nc.vector.memset(a_row[:], 0.0)
            ones = keep.tile([P, P], BF16)
            nc.vector.memset(ones[:], 1.0)
            nc.sync.dma_start(out=a_row[0:1, :], in_=A.rearrange("(one j) i -> one (j i)", one=1))
            for half in range(2):
                a_cols = slice(half * V * V // 2, (half + 1) * V * V // 2)
                a_ps = tw_psum.tile([P, V * V // 2], F32, tag="tw", name="a_ps")
                nc.tensor.matmul(a_ps[:], lhsT=ones[:], rhs=a_row[:, a_cols], start=True, stop=True)
                nc.scalar.copy(out=a_all[:, a_cols], in_=a_ps[:])
            for part in range(1, n_loads):
                load_rel(0, part)
            sort_block(0, [0, 1])
            store_sorted(0, [0, 1])
            nc.vector.tensor_copy(
                out=unsort[:].rearrange("p (w s) -> p s w", s=2), in_=ident[:].rearrange("p (s w) -> p s w", s=2)
            )
            for part in range(n_loads):
                add_static(0, 0, part)
            sort_block(0, [2, 3])
            store_sorted(0, [2, 3])
            for chunk in range(AHEAD):
                load_frames(chunk)
            for part in range(n_loads):
                add_static(0, 1, part)
                for ip in range(2 * part, 2 * part + 2):
                    turn_weights(0, ip)
                    lay_weights(0, ip, False)
            for ip in range(n_ip // 2, n_ip):
                turn_weights(0, ip)
                lay_weights(0, ip, ip % 2 == 1)
                if ip in [13,15]:
                    odd_windows([13,15].index(ip))
                    quantise_windows([13,15].index(ip))

            for s in range(n_groups + 5):
                block, g = divmod(s, groups_in_block)
                inside = s < n_groups
                if s % groups_in_chunk == 0 and s // groups_in_chunk + AHEAD < n_chunks:
                    load_frames(s // groups_in_chunk + AHEAD)
                if s < n_loads:
                    load_rel(1, s)
                if g - 1 in SORT_STEPS and block + 1 < n_blocks:
                    store_sorted(block + 1, [SORT_STEPS.index(g - 1)])
                if max(s + 1, EARLY) < n_groups and s + 1 >= EARLY:
                    odd_windows(s + 1)
                if s >= 1:
                    for ip in turning.get(s - 1, []):
                        lay_weights((s - 1) // groups_in_block + 1, ip, False)
                if 1 <= s <= n_groups:
                    multiply(s - 1)
                for ip in turning.get(s, []):
                    turn_weights(block + 1, ip)
                if EARLY <= s < n_groups:
                    quantise_windows(s)
                if inside:
                    if g < BLOCK // W_CHUNK:
                        quantise_weights(block, g)
                if block == 0 and 2 <= g < 2 + n_loads:
                    add_static(1, 0, g - 2)
                if block == 0 and 2 + n_loads <= g < 2 + 2 * n_loads:
                    add_static(1, 1, g - 2 - n_loads)
                    load_rel(2, g - 2 - n_loads)
                if block == 0 and 2 + 2 * n_loads <= g < 2 + 3 * n_loads:
                    add_static(2, 0, g - 2 - 2 * n_loads)
                if block > 0 and block + 1 < n_blocks and g in SECOND_STEPS:
                    add_static(block + 1, 1, SECOND_STEPS.index(g))
                if block > 0 and block + 2 < n_blocks and g - 1 in SECOND_STEPS:
                    load_rel(block + 2, SECOND_STEPS.index(g - 1))
                if block > 0 and block + 2 < n_blocks and g in FIRST_STEPS:
                    add_static(block + 2, 0, FIRST_STEPS.index(g))
                if 2 <= s < n_groups + 2:
                    collect(s - 2)
                if block > 0 and 3 <= g < 5:
                    for quarter in range(2 * g - 6, 2 * g - 4):
                        spread(block - 1, quarter)
                if block > 0 and 2 <= g < 4:
                    for quarter in range(2 * g - 4, 2 * g - 2):
                        turn(block - 1, quarter)
                if s == 0:
                    load_block(1)
                if g == 12 and block + 2 < n_blocks:
                    load_block(block + 2)
                if g in SORT_STEPS and block + 1 < n_blocks:
                    sort_block(block + 1, [SORT_STEPS.index(g)])
                if block == n_blocks - 1:
                    if g == 0:
                        load_mix()
                    if 6 <= g < 10:
                        lay_mix(g - 6)
                    if 5 <= g < 9:
                        turn_mix(g - 5)
                    if g == 10:
                        quantise_mix()
                        turn_bias()
                    if g == 11:
                        spread_bias()

        zq_pool = stack.enter_context(tc.tile_pool(name="zq", bufs=2))
        y_pool = stack.enter_context(tc.tile_pool(name="y", bufs=6))
        y_psum = stack.enter_context(tc.psum_pool(name="y_ps", bufs=6))
        z_codes_of = {}
        z_scales_of = {}

        def quantise_z(step):
            t_rows = slice(step * T_STEP, (step + 1) * T_STEP)
            z_in = zq_pool.tile([P, N_TILE, PACK], BF16, align_bytes=64)
            nc.vector.tensor_copy(out=z_in[:], in_=z_t[:, :, t_rows, :].rearrange("p r t i -> p (t i) r"))
            z_codes_of[step] = zq_pool.tile([P, N_TILE], U32, align_bytes=64, name="z_codes")
            z_scales_of[step] = zq_pool.tile([P, N_TILE], U8, align_bytes=64, name="z_scales")
            nc.vector.quantize_mx(
                out=z_codes_of[step][:].bitcast(FP8X4),
                scales=z_scales_of[step][:],
                in_=z_in[:].rearrange("p n r -> p (n r)"),
            )

        n_steps = T // T_STEP
        quantise_z(0)
        for step in range(n_steps):
            t_rows = slice(step * T_STEP, (step + 1) * T_STEP)
            if step + 1 < n_steps:
                quantise_z(step + 1)
            for a in range(OUT // P):
                o_cols = slice(a * P, (a + 1) * P)
                y_ps = y_psum.tile([P, N_TILE], F32, tag="y_ps")
                nc.tensor.matmul_mx(
                    out=y_ps[:],
                    lhsT=mix["codes"][:, o_cols].bitcast(FP8X4),
                    lhsT_scale=mix["scales"][:, o_cols],
                    rhs=z_codes_of[step][:].bitcast(FP8X4),
                    rhs_scale=z_scales_of[step][:],
                    start=True,
                    stop=True,
                )
                if a % 2 == 0:
                    y = y_pool.tile([P, 2, N_TILE], F32)
                if a % 3 == 1:
                    nc.vector.tensor_scalar_add(out=y[:, a % 2], in0=y_ps[:], scalar1=b3_cols[:, a : a + 1])
                else:
                    nc.scalar.activation(out=y[:, a % 2], in_=y_ps[:], func=IDENTITY, bias=b3_cols[:, a : a + 1])
                if a % 2 == 1:
                    nc.sync.dma_start(
                        out=out[0, (a - 1) * P : (a + 1) * P, t_rows, :].rearrange("(two p) t i -> p two (t i)", p=P),
                        in_=y[:],
                    )
